import numpy as np
import ml_dtypes


def mxq(x, axis, fmt="e4m3"):
    dtype, down = {"e4m3": (ml_dtypes.float8_e4m3fn, 7), "e5m2": (ml_dtypes.float8_e5m2, 14)}[fmt]
    v = np.moveaxis(np.asarray(x, np.float32).astype(ml_dtypes.bfloat16).astype(np.float64), axis, -1)
    blocks = v.reshape(v.shape[:-1] + (-1, 32))
    amax = np.abs(blocks).max(-1, keepdims=True)
    byte = np.maximum(np.where(amax > 0, np.frexp(amax)[1] - 1 + 127, 0) - down, 1)
    scale = np.exp2(byte - 127.0)
    codes = (blocks / scale).astype(np.float32).astype(dtype).astype(np.float64)
    return np.moveaxis((codes * scale).reshape(v.shape), -1, axis)


WIDE = False


def mx_kscale(k):
    if not WIDE:
        return np.ones(k)
    levels = np.array([10, -10, 5, -5, 0])
    if k % 512:
        return np.exp2(np.random.permutation(np.resize(levels, k // 32))).repeat(32)
    a = np.empty((k // 512, 16))
    for p in range(k // 512):
        a[p, :8] = np.random.permutation(np.resize(levels, 8))
        for g in range(8):
            far = levels[np.abs(levels - a[p, g]) >= 10]
            a[p, g + 8] = far[np.random.randint(len(far))]
    return np.exp2(a.ravel()).repeat(32)


BF16 = ml_dtypes.bfloat16


def bf(x):
    return np.asarray(x, np.float32).astype(BF16)


def f64(x):
    return np.asarray(x).astype(np.float64)


B, N, D, H, DH = 2, 512, 1024, 8, 128
E = H * DH
HALF = DH // 2
EPS = 1e-6
ROPE_BASE = 10000.0
GAIN = np.sqrt(1.8 / DH)


def rmsnorm(t):
    return t * (1.0 / np.sqrt(np.mean(t * t, axis=-1, keepdims=True) + EPS))


def rope(t):
    inv_freq = 1.0 / (ROPE_BASE ** (np.arange(0, DH, 2, dtype=np.float64) / DH))
    ang = np.arange(N, dtype=np.float64)[:, None] * inv_freq[None, :]
    cos, sin = np.cos(ang), np.sin(ang)
    t1, t2 = t[..., :HALF], t[..., HALF:]
    return np.concatenate([t1 * cos - t2 * sin, t1 * sin + t2 * cos], axis=-1)


def heads(t):
    return t.reshape(B, N, H, DH).transpose(0, 2, 1, 3)


def draw0():
    s = mx_kscale(D)
    return {"x": bf(np.random.standard_normal((B, N, D)) * s),
            "w_qkv": bf(np.random.standard_normal((D, 3 * E)) * D ** -0.5 / s[:, None]),
            "scale_param": bf(GAIN * (1.0 + 0.1 * np.random.standard_normal((H, DH))) * D ** -0.5)}


def core(x, w_qkv, scale_param):
    qkv = mxq(f64(x), 2, "e4m3") @ mxq(f64(w_qkv), 0, "e4m3")
    q, k, v = np.split(qkv, 3, axis=-1)
    q, k, v = heads(q), heads(k), heads(v)
    scaler = (f64(scale_param) * (1.0 / (D ** -0.5)))[None, :, None, :]
    q = rmsnorm(q) * scaler
    k = rmsnorm(k) * scaler
    return rope(q), rope(k), v


def e4m3fn_bytes(y):
    return np.clip(np.asarray(y, np.float64), -448.0, 448.0).astype(np.float32).astype(ml_dtypes.float8_e4m3fn).view(np.uint8)


def e4m3fn_values(b):
    return np.asarray(b, np.uint8).view(ml_dtypes.float8_e4m3fn).astype(np.float64)


def setup_inputs():
    d = draw0()
    x0 = np.asarray(d['w_qkv']).astype(np.float64)
    s = (np.max(np.abs(x0), axis=(1,), keepdims=True) / 448.0).astype(np.float32)
    out = {}
    for k, v in d.items():
        if k == 'w_qkv':
            out['w_qkv_bytes'] = e4m3fn_bytes(x0 / s.astype(np.float64))
            out['w_qkv_scale'] = s
        else:
            out[k] = v
    return out


def reference(x, w_qkv_bytes, w_qkv_scale, scale_param):
    return core(x, e4m3fn_values(w_qkv_bytes) * w_qkv_scale.astype(np.float64), scale_param)

@@ -1,0 +1,350 @@
+from contextlib import ExitStack
+
+import concourse.mybir as mybir
+from concourse.masks import make_identity
+
+F32 = mybir.dt.float32
+BF16 = mybir.dt.bfloat16
+U8 = mybir.dt.uint8
+U32 = mybir.dt.uint32
+I32 = mybir.dt.int32
+FP8 = mybir.dt.float8_e4m3fn
+FP8X4 = mybir.dt.float8_e4m3fn_x4
+ACT = mybir.ActivationFunctionType
+ALU = mybir.AluOpType
+
+B, N, D, H, DH = 2, 512, 1024, 8, 128
+E = H * DH
+HALF = DH // 2
+EPS = 1e-6
+ROPE_BASE = 10000.0
+PI = 3.141592653589793
+FLOPS = 2 * B * N * D * 3 * E
+
+P = 128
+PACK = 4
+PASSES = D // (P * PACK)
+CHUNK = 512
+HEADS = CHUNK // DH
+NCHUNK = 3 * E // CHUNK
+TILES = N // P
+BANKS = B * TILES
+NBANK = NCHUNK * BANKS
+
+CHUNK_ORDER = (4, 0, 1, 2, 3, 5)
+ON_VECTOR = (0, 1, 2)
+HEAD_PLACES = 2
+AHEAD_TENSOR = 4
+AHEAD_SCALAR = 2
+LAST_PAIR = (NBANK - BANKS) // 2 - 1
+
+
+def tile_attn_pa_kernel(tc, x, w_qkv_bytes, w_qkv_scale, scale_param, out_0, out_1, out_2):
+    nc = tc.nc
+    outs = (out_0, out_1, out_2)
+
+    with ExitStack() as ctx:
+        keep = ctx.enter_context(tc.tile_pool(name="keep", bufs=1))
+        wide_pool = ctx.enter_context(tc.tile_pool(name="wide", bufs=2))
+        grouped_pool = ctx.enter_context(tc.tile_pool(name="grouped", bufs=2))
+        stats_pool = ctx.enter_context(tc.tile_pool(name="stats", bufs=6))
+        work = ctx.enter_context(tc.tile_pool(name="work", bufs=3))
+        out_pool = ctx.enter_context(tc.tile_pool(name="out", bufs=3))
+        psum = ctx.enter_context(tc.psum_pool(name="psum", bufs=8))
+
+        ctx.enter_context(tc.manual_schedule())
+
+        w_scale = keep.tile([P, PASSES, PACK], F32, name="w_scale")
+        nc.sync.dma_start(out=w_scale[:], in_=w_qkv_scale.rearrange("(g p t) o -> p g (t o)", p=P, t=PACK))
+        gain = keep.tile([P, E], BF16, name="gain")
+        nc.scalar.dma_start(out=gain[:], in_=scale_param.rearrange("h d -> (h d)").partition_broadcast(P))
+        x_raw = [keep.tile([P, TILES, D], BF16, name="x_raw%d" % b) for b in range(B)]
+        bytes_view = w_qkv_bytes.rearrange("(g p t) n -> g p t n", p=P, t=PACK)
+        w_bytes = {}
+
+        def load_x(b):
+            nc.sync.dma_start(out=x_raw[b][:], in_=x[b].rearrange("(r j) k -> r j k", j=TILES))
+
+        def load_w(first, count):
+            for g in range(PASSES):
+                tile8 = keep.tile([P, PACK, count * CHUNK], U8, name="w_bytes%d_%d" % (first, g))
+                nc.sync.dma_start(out=tile8[:], in_=bytes_view[g][:, :, first * CHUNK:(first + count) * CHUNK])
+                for i in range(count):
+                    w_bytes[(first + i, g)] = tile8[:, :, i * CHUNK:(i + 1) * CHUNK]
+
+        load_w(4, 1)
+        load_x(0)
+        load_w(0, 2)
+        load_x(1)
+        load_w(2, 2)
+        load_w(5, 1)
+
+        x_grouped = keep.tile([P, B, PASSES, N, PACK], BF16, name="x_grouped", align_bytes=64)
+        x_codes = keep.tile([P, B, PASSES, N], U32, name="x_codes", align_bytes=64)
+        x_scales = keep.tile([P, B, PASSES, N], U8, name="x_scales", align_bytes=64)
+        w_codes = keep.tile([P, NCHUNK, PASSES, CHUNK], U32, name="w_codes", align_bytes=64)
+        w_scales = keep.tile([P, NCHUNK, PASSES, CHUNK], U8, name="w_scales", align_bytes=64)
+        table = keep.tile([P, TILES, H, 2, DH], F32, name="table")
+
+        wide = {}
+        grouped = {}
+
+        def widen(place, g, t, engine):
+            if place not in wide:
+                wide[place] = wide_pool.tile([P, PASSES, PACK, CHUNK], BF16, name="wide", tag="wide")
+            codes = w_bytes[(CHUNK_ORDER[place], g)][:, t, :].bitcast(FP8)
+            if engine == "scalar":
+                nc.scalar.activation(out=wide[place][:, g, t, :], in_=codes, func=ACT.Copy,
+                                     scale=w_scale[:, g, t:t + 1])
+            else:
+                nc.vector.tensor_scalar(out=wide[place][:, g, t, :], in0=codes, scalar1=w_scale[:, g, t:t + 1],
+                                        scalar2=None, op0=ALU.mult)
+
+        def new_grouped(place):
+            grouped[place] = grouped_pool.tile([P, PASSES, CHUNK, PACK], BF16, name="grouped", tag="grouped",
+                                               align_bytes=64)
+
+        def interleave_on_vector(place):
+            new_grouped(place)
+            nc.vector.tensor_copy(out=grouped[place][:], in_=wide[place][:].rearrange("p g t n -> p g n t"))
+
+        def interleave_on_scalar(place, g):
+            if place not in grouped:
+                new_grouped(place)
+            nc.scalar.copy(out=grouped[place][:, g], in_=wide[place][:, g].rearrange("p t n -> p n t"))
+
+        def quantize_w(place):
+            c = CHUNK_ORDER[place]
+            nc.vector.quantize_mx(out=w_codes[:, c].rearrange("p g n -> p (g n)").bitcast(FP8X4),
+                                  scales=w_scales[:, c].rearrange("p g n -> p (g n)"),
+                                  in_=grouped[place][:].rearrange("p g n t -> p (g n t)"))
+
+        turned = {}
+
+        def transpose_x(b):
+            words = x_raw[b][:].rearrange("r j k -> r (j k)").bitcast(F32)
+            per_token = D // 2
+            per_pass = per_token // PASSES
+            for g in range(PASSES):
+                for pair in range(TILES // 2):
+                    bank = psum.tile([P, 2, 2, P], F32, name="turned", tag="bank")
+                    turned[(b, g, pair)] = bank
+                    for e in range(2):
+                        start = (2 * pair + e) * per_token + g * per_pass
+                        for u in range(2):
+                            nc.tensor.transpose(bank[:, e, u, :], words[:, start + u:start + per_pass:2], ident[:])
+
+        def copy_x(b):
+            for g in range(PASSES):
+                for pair in range(TILES // 2):
+                    cols = x_grouped[:, b, g, 2 * pair * P:2 * (pair + 1) * P, :]
+                    cols = cols.rearrange("p c t -> p (c t)").bitcast(F32)
+                    nc.scalar.copy(out=cols.rearrange("p (e r u) -> p e r u", e=2, u=2),
+                                   in_=turned[(b, g, pair)][:].rearrange("p e u r -> p e r u"))
+
+        def quantize_x(b):
+            nc.vector.quantize_mx(out=x_codes[:, b].rearrange("p g c -> p (g c)").bitcast(FP8X4),
+                                  scales=x_scales[:, b].rearrange("p g c -> p (g c)"),
+                                  in_=x_grouped[:, b].rearrange("p g c t -> p (g c t)"))
+
+        position_i = keep.tile([P, TILES], I32, name="position_i")
+        nc.gpsimd.iota(position_i[:], pattern=[[1, TILES]], base=0, channel_multiplier=TILES)
+        zero = keep.tile([P, 1], F32, name="zero")
+        nc.gpsimd.memset(zero[:], 0.0)
+        ident = keep.tile([P, P], F32, name="ident")
+        make_identity(nc, ident[:])
+        unused = keep.tile([P, 1], F32, name="unused")
+        nc.scalar.activation(out=unused[:], in_=zero[:], func=ACT.Sin)
+
+        position = keep.tile([P, TILES], F32, name="position")
+        nc.vector.tensor_copy(out=position[:], in_=position_i[:])
+        freq = keep.tile([P, HALF], F32, name="freq")
+        nc.vector.memset(freq[:, 0:1], 1.0)
+        width = 1
+        while width < HALF:
+            nc.vector.tensor_scalar(out=freq[:, width:2 * width], in0=freq[:, 0:width],
+                                    scalar1=ROPE_BASE ** (-width / HALF), scalar2=None, op0=ALU.mult)
+            width *= 2
+        angle = keep.tile([P, TILES, HALF], F32, name="angle")
+        nc.vector.tensor_tensor(out=angle[:], in0=position[:].unsqueeze(2).to_broadcast([P, TILES, HALF]),
+                                in1=freq[:].unsqueeze(1).to_broadcast([P, TILES, HALF]), op=ALU.mult)
+        turns = keep.tile([P, 2, TILES, HALF], F32, name="turns")
+        nc.vector.tensor_scalar(out=turns[:, 0], in0=angle[:], scalar1=0.5 / PI, scalar2=0.5,
+                                op0=ALU.mult, op1=ALU.add)
+        nc.vector.tensor_scalar(out=turns[:, 1], in0=angle[:], scalar1=0.5 / PI, scalar2=0.75,
+                                op0=ALU.mult, op1=ALU.add)
+        whole_i = keep.tile([P, 2, TILES, HALF], I32, name="whole_i")
+        nc.vector.tensor_copy(out=whole_i[:], in_=turns[:])
+        whole = keep.tile([P, 2, TILES, HALF], F32, name="whole")
+        nc.vector.tensor_copy(out=whole[:], in_=whole_i[:])
+        part = keep.tile([P, 2, TILES, HALF], F32, name="part")
+        nc.vector.tensor_tensor(out=part[:], in0=turns[:], in1=whole[:], op=ALU.subtract)
+        flat = "p a j f -> p (a j f)"
+        part01 = keep.tile([P, 2, TILES, HALF], F32, name="part01")
+        nc.vector.scalar_tensor_tensor(out=part01[:].rearrange(flat), in0=part[:].rearrange(flat), scalar=0.0,
+                                       in1=part[:].rearrange(flat), op0=ALU.is_lt, op1=ALU.add)
+        reduced = keep.tile([P, 2, TILES, HALF], F32, name="reduced")
+        nc.vector.tensor_scalar(out=reduced[:], in0=part01[:], scalar1=2.0 * PI, scalar2=-PI,
+                                op0=ALU.mult, op1=ALU.add)
+
+        for t in range(PACK):
+            widen(0, 0, t, "scalar")
+            widen(0, 1, t, "vector")
+        trig = keep.tile([P, TILES, 2, 2, HALF], F32, name="trig")
+        nc.scalar.activation(out=trig[:, :, 0, 0, :], in_=reduced[:, 1], func=ACT.Sin)
+        nc.scalar.activation(out=trig[:, :, 0, 1, :], in_=reduced[:, 1], func=ACT.Sin)
+        nc.scalar.activation(out=trig[:, :, 1, 0, :], in_=reduced[:, 0], func=ACT.Sin)
+        nc.scalar.activation(out=trig[:, :, 1, 1, :], in_=reduced[:, 0], func=ACT.Sin, scale=-1.0)
+        nc.scalar.activation(out=unused[:], in_=zero[:], func=ACT.Abs_reciprocal_sqrt, bias=1.0)
+
+        def build_table(j):
+            for a in range(2):
+                nc.vector.tensor_tensor(out=table[:, j, :, a, :], in0=gain[:].rearrange("p (h d) -> p h d", d=DH),
+                                        in1=trig[:, j, a].rearrange("p s f -> p (s f)").unsqueeze(1).to_broadcast([P, H, DH]),
+                                        op=ALU.mult)
+
+        transpose_x(0)
+        copy_x(0)
+        transpose_x(1)
+        copy_x(1)
+        for g in range(PASSES):
+            for t in range(PACK):
+                widen(1, g, t, "scalar")
+        interleave_on_vector(0)
+        build_table(0)
+        quantize_x(0)
+        quantize_w(0)
+        build_table(1)
+        quantize_x(1)
+        build_table(2)
+        interleave_on_vector(1)
+        build_table(3)
+        quantize_w(1)
+
+        sums, rstds, products, results = {}, {}, {}, {}
+
+        def where(s):
+            return CHUNK_ORDER[s // BANKS], (s % BANKS) // TILES, s % TILES
+
+        def multiply(s):
+            c, b, j = where(s)
+            sums[s] = psum.tile([P, CHUNK], F32, name="sums", tag="bank")
+            for g in range(PASSES):
+                nc.tensor.matmul_mx(out=sums[s][:], lhsT=x_codes[:, b, g, j * P:(j + 1) * P].bitcast(FP8X4),
+                                    lhsT_scale=x_scales[:, b, g, j * P:(j + 1) * P],
+                                    rhs=w_codes[:, c, g, :].bitcast(FP8X4), rhs_scale=w_scales[:, c, g, :],
+                                    start=(g == 0), stop=(g == PASSES - 1))
+
+        def result_tile(s):
+            if s // TILES not in results:
+                results[s // TILES] = out_pool.tile([P, HEADS, TILES, DH], F32, name="result", tag="result")
+            return results[s // TILES]
+
+        def store(s):
+            c, b, j = where(s)
+            first_head = (c % 2) * HEADS
+            rows = outs[c // 2][b, first_head:first_head + HEADS].rearrange("h (r j) d -> r h j d", j=TILES)
+            result = results[s // TILES]
+            if s // TILES == NBANK // TILES - 1:
+                nc.scalar.dma_start(out=rows[:, :, j, :], in_=result[:, :, j, :])
+            elif s // 2 == LAST_PAIR:
+                nc.sync.dma_start(out=rows[:, :, j, :], in_=result[:, :, j, :])
+            elif c // 2 != 2 and j % 2 == 1:
+                nc.sync.dma_start(out=rows[:, :, j - 1:j + 1, :].rearrange("r h j d -> r h (j d)"),
+                                  in_=result[:, :, j - 1:j + 1, :].rearrange("r h j d -> r h (j d)"))
+            elif c // 2 == 2 and j == TILES - 1:
+                nc.scalar.dma_start(out=rows.rearrange("r h j d -> r h (j d)"),
+                                    in_=result[:].rearrange("r h j d -> r h (j d)"))
+
+        def scalar_reads(s):
+            c, b, j = where(s)
+            if c // 2 == 2:
+                nc.scalar.copy(out=result_tile(s)[:, :, j, :], in_=sums[s][:].rearrange("p (h d) -> p h d", d=DH))
+                store(s)
+                return
+            square_sum = stats_pool.tile([P, HEADS], F32, name="square_sum", tag="square_sum")
+            for h in range(HEADS):
+                squares = work.tile([P, DH], BF16, name="squares", tag="squares")
+                nc.scalar.activation(out=squares[:], in_=sums[s][:, h * DH:(h + 1) * DH], func=ACT.Square,
+                                     accum_out=square_sum[:, h:h + 1])
+            rstds[s] = stats_pool.tile([P, HEADS], F32, name="rstd", tag="rstd")
+            nc.scalar.activation(out=rstds[s][:], in_=square_sum[:], func=ACT.Abs_reciprocal_sqrt,
+                                 scale=1.0 / (DH * D), bias=EPS / D)
+
+        def vector_multiplies(s):
+            c, b, j = where(s)
+            if c // 2 == 2:
+                return
+            first_head = (c % 2) * HEADS
+            if s // 2 not in products:
+                products[s // 2] = work.tile([P, 2, HEADS, 2, 2, HALF], F32, name="products", tag="products")
+            for h in range(HEADS):
+                nc.vector.scalar_tensor_tensor(
+                    out=products[s // 2][:, s % 2, h].rearrange("p a s f -> p a (s f)"),
+                    in0=table[:, j, first_head + h], scalar=rstds[s][:, h:h + 1],
+                    in1=sums[s][:, h * DH:(h + 1) * DH].unsqueeze(1).to_broadcast([P, 2, DH]),
+                    op0=ALU.mult, op1=ALU.mult)
+
+        def vector_sums(s):
+            c, b, j = where(s)
+            if c // 2 == 2:
+                return
+            result = result_tile(s)
+            if s // 2 == LAST_PAIR:
+                pair = products[s // 2][:, s % 2]
+                for low in range(2):
+                    nc.vector.tensor_tensor(out=result[:, :, j, low * HALF:(low + 1) * HALF],
+                                            in0=pair[:, :, 0, low, :], in1=pair[:, :, 1, 1 - low, :], op=ALU.add)
+                store(s)
+                return
+            if s % 2 == 0:
+                return
+            pair = products[s // 2][:].rearrange("p e h a s f -> p h e a s f")
+            for low in range(2):
+                nc.vector.tensor_tensor(out=result[:, :, j - 1:j + 1, low * HALF:(low + 1) * HALF],
+                                        in0=pair[:, :, :, 0, low, :], in1=pair[:, :, :, 1, 1 - low, :], op=ALU.add)
+            store(s)
+
+        pieces = []
+        for place in range(HEAD_PLACES, NCHUNK):
+            for g in range(PASSES):
+                for t in range(PACK):
+                    pieces.append(("widen", place, g, t))
+                if place not in ON_VECTOR:
+                    pieces.append(("interleave", place, g, 0))
+            pieces.append(("widened", place, 0, 0))
+        taken = 0
+        vector_later = {}
+        quantized = set(range(HEAD_PLACES))
+
+        for s in range(-AHEAD_TENSOR, NBANK + 1):
+            if 0 <= s + AHEAD_TENSOR < NBANK:
+                assert (s + AHEAD_TENSOR) // BANKS in quantized
+                multiply(s + AHEAD_TENSOR)
+            if 0 <= s + AHEAD_SCALAR < NBANK:
+                scalar_reads(s + AHEAD_SCALAR)
+            if 0 <= s < NBANK:
+                planes = 1
+                while taken < len(pieces) and (planes > 0 or pieces[taken][0] != "widen"):
+                    kind, place, g, t = pieces[taken]
+                    taken += 1
+                    if kind == "widen":
+                        widen(place, g, t, "scalar")
+                        planes -= 1
+                    elif kind == "interleave":
+                        interleave_on_scalar(place, g)
+                    elif place in ON_VECTOR:
+                        vector_later[s + 1] = ("interleave", place)
+                        vector_later[s + 3] = ("quantize", place)
+                    else:
+                        vector_later[s + 2] = ("quantize", place)
+                vector_multiplies(s)
+                if s in vector_later:
+                    kind, place = vector_later[s]
+                    if kind == "interleave":
+                        interleave_on_vector(place)
+                    else:
+                        quantize_w(place)
+                        quantized.add(place)
+            if 0 <= s - 1:
+                vector_sums(s - 1)

@@ -36,6 +36,7 @@ ON_VECTOR = (0, 1, 2)
 HEAD_PLACES = 2
 AHEAD_TENSOR = 4
 AHEAD_SCALAR = 2
+RUN = 4
 LAST_PAIR = (NBANK - BANKS) // 2 - 1
 
 
@@ -106,12 +107,15 @@ def tile_attn_pa_kernel(tc, x, w_qkv_bytes, w_qkv_scale, scale_param, out_0, out
 
         def interleave_on_vector(place):
             new_grouped(place)
-            nc.vector.tensor_copy(out=grouped[place][:], in_=wide[place][:].rearrange("p g t n -> p g n t"))
+            for g in range(PASSES):
+                nc.vector.tensor_copy(out=grouped[place][:, g].rearrange("p (c i) t -> p c t i", i=RUN),
+                                      in_=wide[place][:, g].rearrange("p t (c i) -> p c t i", i=RUN))
 
         def interleave_on_scalar(place, g):
             if place not in grouped:
                 new_grouped(place)
-            nc.scalar.copy(out=grouped[place][:, g], in_=wide[place][:, g].rearrange("p t n -> p n t"))
+            nc.scalar.copy(out=grouped[place][:, g].rearrange("p (c i) t -> p c t i", i=RUN),
+                           in_=wide[place][:, g].rearrange("p t (c i) -> p c t i", i=RUN))
 
         def quantize_w(place):
             c = CHUNK_ORDER[place]

@@ -32,7 +32,7 @@ BANKS = B * TILES
 NBANK = NCHUNK * BANKS
 
 CHUNK_ORDER = (4, 0, 1, 2, 3, 5)
-ON_VECTOR = (0, 1, 2)
+ON_VECTOR = (0, 1, 2, 3)
 HEAD_PLACES = 2
 AHEAD_TENSOR = 4
 AHEAD_SCALAR = 2

@@ -34,8 +34,8 @@ NBANK = NCHUNK * BANKS
 CHUNK_ORDER = (4, 0, 1, 2, 3, 5)
 ON_VECTOR = (0, 1, 2, 3)
 HEAD_PLACES = 2
-AHEAD_TENSOR = 4
-AHEAD_SCALAR = 2
+AHEAD_TENSOR = 5
+AHEAD_SCALAR = 3
 RUN = 4
 LAST_PAIR = (NBANK - BANKS) // 2 - 1
 
@@ -196,9 +196,9 @@ def tile_attn_pa_kernel(tc, x, w_qkv_bytes, w_qkv_scale, scale_param, out_0, out
             widen(0, 1, t, "vector")
         trig = keep.tile([P, TILES, 2, 2, HALF], F32, name="trig")
         nc.scalar.activation(out=trig[:, :, 0, 0, :], in_=reduced[:, 1], func=ACT.Sin)
-        nc.scalar.activation(out=trig[:, :, 0, 1, :], in_=reduced[:, 1], func=ACT.Sin)
+        nc.scalar.activation(out=trig[:, :, 1, 1, :], in_=reduced[:, 1], func=ACT.Sin)
         nc.scalar.activation(out=trig[:, :, 1, 0, :], in_=reduced[:, 0], func=ACT.Sin)
-        nc.scalar.activation(out=trig[:, :, 1, 1, :], in_=reduced[:, 0], func=ACT.Sin, scale=-1.0)
+        nc.scalar.activation(out=trig[:, :, 0, 1, :], in_=reduced[:, 0], func=ACT.Sin, scale=-1.0)
         nc.scalar.activation(out=unused[:], in_=zero[:], func=ACT.Abs_reciprocal_sqrt, bias=1.0)
 
         def build_table(j):
@@ -225,7 +225,7 @@ def tile_attn_pa_kernel(tc, x, w_qkv_bytes, w_qkv_scale, scale_param, out_0, out
         build_table(3)
         quantize_w(1)
 
-        sums, rstds, products, results = {}, {}, {}, {}
+        sums, square_sums, rstds, products, results = {}, {}, {}, {}, {}
 
         def where(s):
             return CHUNK_ORDER[s // BANKS], (s % BANKS) // TILES, s % TILES
@@ -266,13 +266,16 @@ def tile_attn_pa_kernel(tc, x, w_qkv_bytes, w_qkv_scale, scale_param, out_0, out
                 nc.scalar.copy(out=result_tile(s)[:, :, j, :], in_=sums[s][:].rearrange("p (h d) -> p h d", d=DH))
                 store(s)
                 return
-            square_sum = stats_pool.tile([P, HEADS], F32, name="square_sum", tag="square_sum")
+            if s % 2 == 0:
+                square_sums[s // 2] = stats_pool.tile([P, 2, HEADS], F32, name="square_sum", tag="square_sum")
             for h in range(HEADS):
                 squares = work.tile([P, DH], BF16, name="squares", tag="squares")
                 nc.scalar.activation(out=squares[:], in_=sums[s][:, h * DH:(h + 1) * DH], func=ACT.Square,
-                                     accum_out=square_sum[:, h:h + 1])
-            rstds[s] = stats_pool.tile([P, HEADS], F32, name="rstd", tag="rstd")
-            nc.scalar.activation(out=rstds[s][:], in_=square_sum[:], func=ACT.Abs_reciprocal_sqrt,
+                                     accum_out=square_sums[s // 2][:, s % 2, h:h + 1])
+            if s % 2 == 0:
+                return
+            rstds[s // 2] = stats_pool.tile([P, 2, HEADS], F32, name="rstd", tag="rstd")
+            nc.scalar.activation(out=rstds[s // 2][:], in_=square_sums[s // 2][:], func=ACT.Abs_reciprocal_sqrt,
                                  scale=1.0 / (DH * D), bias=EPS / D)
 
         def vector_multiplies(s):
@@ -285,7 +288,7 @@ def tile_attn_pa_kernel(tc, x, w_qkv_bytes, w_qkv_scale, scale_param, out_0, out
             for h in range(HEADS):
                 nc.vector.scalar_tensor_tensor(
                     out=products[s // 2][:, s % 2, h].rearrange("p a s f -> p a (s f)"),
-                    in0=table[:, j, first_head + h], scalar=rstds[s][:, h:h + 1],
+                    in0=table[:, j, first_head + h], scalar=rstds[s // 2][:, s % 2, h:h + 1],
                     in1=sums[s][:, h * DH:(h + 1) * DH].unsqueeze(1).to_broadcast([P, 2, DH]),
                     op0=ALU.mult, op1=ALU.mult)
 
@@ -295,18 +298,16 @@ def tile_attn_pa_kernel(tc, x, w_qkv_bytes, w_qkv_scale, scale_param, out_0, out
                 return
             result = result_tile(s)
             if s // 2 == LAST_PAIR:
-                pair = products[s // 2][:, s % 2]
-                for low in range(2):
-                    nc.vector.tensor_tensor(out=result[:, :, j, low * HALF:(low + 1) * HALF],
-                                            in0=pair[:, :, 0, low, :], in1=pair[:, :, 1, 1 - low, :], op=ALU.add)
+                one = products[s // 2][:, s % 2]
+                nc.vector.tensor_tensor(out=result[:, :, j, :].rearrange("p h (o f) -> p h o f", f=HALF),
+                                        in0=one[:, :, :, 0, :], in1=one[:, :, :, 1, :], op=ALU.add)
                 store(s)
                 return
             if s % 2 == 0:
                 return
-            pair = products[s // 2][:].rearrange("p e h a s f -> p h e a s f")
-            for low in range(2):
-                nc.vector.tensor_tensor(out=result[:, :, j - 1:j + 1, low * HALF:(low + 1) * HALF],
-                                        in0=pair[:, :, :, 0, low, :], in1=pair[:, :, :, 1, 1 - low, :], op=ALU.add)
+            pair = products[s // 2]
+            nc.vector.tensor_tensor(out=result[:, :, j - 1:j + 1, :].rearrange("p h e (o f) -> p e h o f", f=HALF),
+                                    in0=pair[:, :, :, :, 0, :], in1=pair[:, :, :, :, 1, :], op=ALU.add)
             store(s)
 
         pieces = []

@@ -32,7 +32,7 @@ BANKS = B * TILES
 NBANK = NCHUNK * BANKS
 
 CHUNK_ORDER = (4, 0, 1, 2, 3, 5)
-ON_VECTOR = (0, 1, 2, 3)
+ON_VECTOR = (0, 1, 2, 3, 4, 5)
 HEAD_PLACES = 2
 AHEAD_TENSOR = 5
 AHEAD_SCALAR = 3
@@ -306,7 +306,7 @@ def tile_attn_pa_kernel(tc, x, w_qkv_bytes, w_qkv_scale, scale_param, out_0, out
             if s % 2 == 0:
                 return
             pair = products[s // 2]
-            nc.vector.tensor_tensor(out=result[:, :, j - 1:j + 1, :].rearrange("p h e (o f) -> p e h o f", f=HALF),
+            nc.gpsimd.tensor_tensor(out=result[:, :, j - 1:j + 1, :].rearrange("p h e (o f) -> p e h o f", f=HALF),
                                     in0=pair[:, :, :, :, 0, :], in1=pair[:, :, :, :, 1, :], op=ALU.add)
             store(s)
 

@@ -26,18 +26,12 @@ PACK = 4
 PASSES = D // (P * PACK)
 CHUNK = 512
 HEADS = CHUNK // DH
-NCHUNK = 3 * E // CHUNK
 TILES = N // P
-BANKS = B * TILES
-NBANK = NCHUNK * BANKS
-
-CHUNK_ORDER = (4, 0, 1, 2, 3, 5)
-ON_VECTOR = (0, 1, 2, 3, 4, 5)
-HEAD_PLACES = 2
-AHEAD_TENSOR = 5
-AHEAD_SCALAR = 3
+UNITS = 3
+Q, K, V = 0, 1, 2
 RUN = 4
-LAST_PAIR = (NBANK - BANKS) // 2 - 1
+AHEAD_TENSOR = 7
+AHEAD_SCALAR = 5
 
 
 def tile_attn_pa_kernel(tc, x, w_qkv_bytes, w_qkv_scale, scale_param, out_0, out_1, out_2):
@@ -46,11 +40,11 @@ def tile_attn_pa_kernel(tc, x, w_qkv_bytes, w_qkv_scale, scale_param, out_0, out
 
     with ExitStack() as ctx:
         keep = ctx.enter_context(tc.tile_pool(name="keep", bufs=1))
-        wide_pool = ctx.enter_context(tc.tile_pool(name="wide", bufs=2))
-        grouped_pool = ctx.enter_context(tc.tile_pool(name="grouped", bufs=2))
+        stage = ctx.enter_context(tc.tile_pool(name="stage", bufs=4))
+        plane_pool = ctx.enter_context(tc.tile_pool(name="flat", bufs=3))
+        v_pool = ctx.enter_context(tc.tile_pool(name="v_out", bufs=2))
         stats_pool = ctx.enter_context(tc.tile_pool(name="stats", bufs=6))
-        work = ctx.enter_context(tc.tile_pool(name="work", bufs=3))
-        out_pool = ctx.enter_context(tc.tile_pool(name="out", bufs=3))
+        scrap = ctx.enter_context(tc.tile_pool(name="scrap", bufs=3))
         psum = ctx.enter_context(tc.psum_pool(name="psum", bufs=8))
 
         ctx.enter_context(tc.manual_schedule())
@@ -66,62 +60,45 @@ def tile_attn_pa_kernel(tc, x, w_qkv_bytes, w_qkv_scale, scale_param, out_0, out
         def load_x(b):
             nc.sync.dma_start(out=x_raw[b][:], in_=x[b].rearrange("(r j) k -> r j k", j=TILES))
 
-        def load_w(first, count):
+        def load_w(u):
             for g in range(PASSES):
-                tile8 = keep.tile([P, PACK, count * CHUNK], U8, name="w_bytes%d_%d" % (first, g))
-                nc.sync.dma_start(out=tile8[:], in_=bytes_view[g][:, :, first * CHUNK:(first + count) * CHUNK])
-                for i in range(count):
-                    w_bytes[(first + i, g)] = tile8[:, :, i * CHUNK:(i + 1) * CHUNK]
+                w_bytes[(u, g)] = keep.tile([P, PACK, E], U8, name="w_bytes%d_%d" % (u, g))
+                nc.sync.dma_start(out=w_bytes[(u, g)][:], in_=bytes_view[g][:, :, u * E:(u + 1) * E])
 
-        load_w(4, 1)
+        load_w(Q)
         load_x(0)
-        load_w(0, 2)
         load_x(1)
-        load_w(2, 2)
-        load_w(5, 1)
+        load_w(K)
+        load_w(V)
 
         x_grouped = keep.tile([P, B, PASSES, N, PACK], BF16, name="x_grouped", align_bytes=64)
         x_codes = keep.tile([P, B, PASSES, N], U32, name="x_codes", align_bytes=64)
         x_scales = keep.tile([P, B, PASSES, N], U8, name="x_scales", align_bytes=64)
-        w_codes = keep.tile([P, NCHUNK, PASSES, CHUNK], U32, name="w_codes", align_bytes=64)
-        w_scales = keep.tile([P, NCHUNK, PASSES, CHUNK], U8, name="w_scales", align_bytes=64)
+        w_codes = keep.tile([P, UNITS, PASSES, E], U32, name="w_codes", align_bytes=64)
+        w_scales = keep.tile([P, UNITS, PASSES, E], U8, name="w_scales", align_bytes=64)
         table = keep.tile([P, TILES, H, 2, DH], F32, name="table")
 
         wide = {}
         grouped = {}
 
-        def widen(place, g, t, engine):
-            if place not in wide:
-                wide[place] = wide_pool.tile([P, PASSES, PACK, CHUNK], BF16, name="wide", tag="wide")
-            codes = w_bytes[(CHUNK_ORDER[place], g)][:, t, :].bitcast(FP8)
+        def widen(u, g, t, engine):
+            if (u, g) not in wide:
+                wide[(u, g)] = stage.tile([P, PACK, E], BF16, name="wide", tag="stage")
+            codes = w_bytes[(u, g)][:, t, :].bitcast(FP8)
             if engine == "scalar":
-                nc.scalar.activation(out=wide[place][:, g, t, :], in_=codes, func=ACT.Copy,
-                                     scale=w_scale[:, g, t:t + 1])
+                nc.scalar.activation(out=wide[(u, g)][:, t, :], in_=codes, func=ACT.Copy, scale=w_scale[:, g, t:t + 1])
             else:
-                nc.vector.tensor_scalar(out=wide[place][:, g, t, :], in0=codes, scalar1=w_scale[:, g, t:t + 1],
+                nc.vector.tensor_scalar(out=wide[(u, g)][:, t, :], in0=codes, scalar1=w_scale[:, g, t:t + 1],
                                         scalar2=None, op0=ALU.mult)
 
-        def new_grouped(place):
-            grouped[place] = grouped_pool.tile([P, PASSES, CHUNK, PACK], BF16, name="grouped", tag="grouped",
-                                               align_bytes=64)
+        def interleave(u, g):
+            grouped[(u, g)] = plane_pool.tile([P, E, PACK], BF16, name="grouped", tag="flat", align_bytes=64)
+            nc.vector.tensor_copy(out=grouped[(u, g)][:].rearrange("p (c i) t -> p c t i", i=RUN),
+                                  in_=wide[(u, g)][:].rearrange("p t (c i) -> p c t i", i=RUN))
 
-        def interleave_on_vector(place):
-            new_grouped(place)
-            for g in range(PASSES):
-                nc.vector.tensor_copy(out=grouped[place][:, g].rearrange("p (c i) t -> p c t i", i=RUN),
-                                      in_=wide[place][:, g].rearrange("p t (c i) -> p c t i", i=RUN))
-
-        def interleave_on_scalar(place, g):
-            if place not in grouped:
-                new_grouped(place)
-            nc.scalar.copy(out=grouped[place][:, g].rearrange("p (c i) t -> p c t i", i=RUN),
-                           in_=wide[place][:, g].rearrange("p t (c i) -> p c t i", i=RUN))
-
-        def quantize_w(place):
-            c = CHUNK_ORDER[place]
-            nc.vector.quantize_mx(out=w_codes[:, c].rearrange("p g n -> p (g n)").bitcast(FP8X4),
-                                  scales=w_scales[:, c].rearrange("p g n -> p (g n)"),
-                                  in_=grouped[place][:].rearrange("p g n t -> p (g n t)"))
+        def quantize_w(u, g):
+            nc.vector.quantize_mx(out=w_codes[:, u, g, :].bitcast(FP8X4), scales=w_scales[:, u, g, :],
+                                  in_=grouped[(u, g)][:].rearrange("p n t -> p (n t)"))
 
         turned = {}
 
@@ -191,9 +168,10 @@ def tile_attn_pa_kernel(tc, x, w_qkv_bytes, w_qkv_scale, scale_param, out_0, out
         nc.vector.tensor_scalar(out=reduced[:], in0=part01[:], scalar1=2.0 * PI, scalar2=-PI,
                                 op0=ALU.mult, op1=ALU.add)
 
+
         for t in range(PACK):
-            widen(0, 0, t, "scalar")
-            widen(0, 1, t, "vector")
+            widen(Q, 0, t, "scalar")
+            widen(Q, 1, t, "vector")
         trig = keep.tile([P, TILES, 2, 2, HALF], F32, name="trig")
         nc.scalar.activation(out=trig[:, :, 0, 0, :], in_=reduced[:, 1], func=ACT.Sin)
         nc.scalar.activation(out=trig[:, :, 1, 1, :], in_=reduced[:, 1], func=ACT.Sin)
@@ -202,154 +180,126 @@ def tile_attn_pa_kernel(tc, x, w_qkv_bytes, w_qkv_scale, scale_param, out_0, out
         nc.scalar.activation(out=unused[:], in_=zero[:], func=ACT.Abs_reciprocal_sqrt, bias=1.0)
 
         def build_table(j):
-            for a in range(2):
-                nc.vector.tensor_tensor(out=table[:, j, :, a, :], in0=gain[:].rearrange("p (h d) -> p h d", d=DH),
-                                        in1=trig[:, j, a].rearrange("p s f -> p (s f)").unsqueeze(1).to_broadcast([P, H, DH]),
+            for o in range(2):
+                nc.vector.tensor_tensor(out=table[:, j, :, o, :], in0=gain[:].rearrange("p (h d) -> p h d", d=DH),
+                                        in1=trig[:, j, o].rearrange("p i f -> p (i f)").unsqueeze(1).to_broadcast([P, H, DH]),
                                         op=ALU.mult)
 
         transpose_x(0)
         copy_x(0)
         transpose_x(1)
         copy_x(1)
-        for g in range(PASSES):
-            for t in range(PACK):
-                widen(1, g, t, "scalar")
-        interleave_on_vector(0)
+        interleave(Q, 1)
+        interleave(Q, 0)
+        quantize_w(Q, 1)
+        quantize_w(Q, 0)
         build_table(0)
-        quantize_x(0)
-        quantize_w(0)
         build_table(1)
-        quantize_x(1)
+        quantize_x(0)
         build_table(2)
-        interleave_on_vector(1)
+        quantize_x(1)
         build_table(3)
-        quantize_w(1)
+        for u in (K, V):
+            for g in range(PASSES):
+                for t in range(PACK):
+                    widen(u, g, t, "scalar")
+            interleave(u, 0)
+            interleave(u, 1)
+            quantize_w(u, 0)
+            quantize_w(u, 1)
 
+        rotated = [(c, b, j) for c in range(4) for b in range(B) for j in range(TILES)]
+        plain = [(c, b, j) for c in (4, 5) for b in range(B) for j in range(TILES)]
+        order = []
+        for i in range(len(plain)):
+            order.extend([plain[i], rotated[2 * i], rotated[2 * i + 1]])
+        LAST = len(order) - 1
         sums, square_sums, rstds, products, results = {}, {}, {}, {}, {}
 
-        def where(s):
-            return CHUNK_ORDER[s // BANKS], (s % BANKS) // TILES, s % TILES
-
         def multiply(s):
-            c, b, j = where(s)
+            c, b, j = order[s]
+            columns = slice((c % 2) * CHUNK, (c % 2 + 1) * CHUNK)
             sums[s] = psum.tile([P, CHUNK], F32, name="sums", tag="bank")
             for g in range(PASSES):
                 nc.tensor.matmul_mx(out=sums[s][:], lhsT=x_codes[:, b, g, j * P:(j + 1) * P].bitcast(FP8X4),
                                     lhsT_scale=x_scales[:, b, g, j * P:(j + 1) * P],
-                                    rhs=w_codes[:, c, g, :].bitcast(FP8X4), rhs_scale=w_scales[:, c, g, :],
+                                    rhs=w_codes[:, c // 2, g, columns].bitcast(FP8X4),
+                                    rhs_scale=w_scales[:, c // 2, g, columns],
                                     start=(g == 0), stop=(g == PASSES - 1))
 
-        def result_tile(s):
-            if s // TILES not in results:
-                results[s // TILES] = out_pool.tile([P, HEADS, TILES, DH], F32, name="result", tag="result")
-            return results[s // TILES]
-
-        def store(s):
-            c, b, j = where(s)
+        def rows_of(c, b):
             first_head = (c % 2) * HEADS
-            rows = outs[c // 2][b, first_head:first_head + HEADS].rearrange("h (r j) d -> r h j d", j=TILES)
-            result = results[s // TILES]
-            if s // TILES == NBANK // TILES - 1:
-                nc.scalar.dma_start(out=rows[:, :, j, :], in_=result[:, :, j, :])
-            elif s // 2 == LAST_PAIR:
-                nc.sync.dma_start(out=rows[:, :, j, :], in_=result[:, :, j, :])
-            elif c // 2 != 2 and j % 2 == 1:
-                nc.sync.dma_start(out=rows[:, :, j - 1:j + 1, :].rearrange("r h j d -> r h (j d)"),
-                                  in_=result[:, :, j - 1:j + 1, :].rearrange("r h j d -> r h (j d)"))
-            elif c // 2 == 2 and j == TILES - 1:
-                nc.scalar.dma_start(out=rows.rearrange("r h j d -> r h (j d)"),
-                                    in_=result[:].rearrange("r h j d -> r h (j d)"))
+            return outs[c // 2][b, first_head:first_head + HEADS].rearrange("h (r j) d -> r h j d", j=TILES)
+
+        def copy_v(s, engine):
+            c, b, j = order[s]
+            if j == 0:
+                results[(c, b)] = v_pool.tile([P, HEADS, TILES, DH], F32, name="v_result", tag="v_result")
+            result = results[(c, b)]
+            if engine == "scalar":
+                nc.scalar.copy(out=result[:, :, j, :], in_=sums[s][:].rearrange("p (h d) -> p h d", d=DH))
+            else:
+                nc.vector.tensor_copy(out=result[:, :, j, :], in_=sums[s][:].rearrange("p (h d) -> p h d", d=DH))
+            if j == TILES - 1:
+                nc.sync.dma_start(out=rows_of(c, b).rearrange("r h j d -> r h (j d)"),
+                                  in_=result[:].rearrange("r h j d -> r h (j d)"))
 
         def scalar_reads(s):
-            c, b, j = where(s)
-            if c // 2 == 2:
-                nc.scalar.copy(out=result_tile(s)[:, :, j, :], in_=sums[s][:].rearrange("p (h d) -> p h d", d=DH))
-                store(s)
+            c, b, j = order[s]
+            if c // 2 == V:
+                if j % 2 == 0:
+                    copy_v(s, "scalar")
                 return
-            if s % 2 == 0:
-                square_sums[s // 2] = stats_pool.tile([P, 2, HEADS], F32, name="square_sum", tag="square_sum")
+            pair = (c, b, j // 2)
+            if j % 2 == 0:
+                square_sums[pair] = stats_pool.tile([P, 2, HEADS], F32, name="square_sum", tag="square_sum")
             for h in range(HEADS):
-                squares = work.tile([P, DH], BF16, name="squares", tag="squares")
+                squares = scrap.tile([P, DH], BF16, name="squares", tag="squares")
                 nc.scalar.activation(out=squares[:], in_=sums[s][:, h * DH:(h + 1) * DH], func=ACT.Square,
-                                     accum_out=square_sums[s // 2][:, s % 2, h:h + 1])
-            if s % 2 == 0:
+                                     accum_out=square_sums[pair][:, j % 2, h:h + 1])
+            if j % 2 == 0:
                 return
-            rstds[s // 2] = stats_pool.tile([P, 2, HEADS], F32, name="rstd", tag="rstd")
-            nc.scalar.activation(out=rstds[s // 2][:], in_=square_sums[s // 2][:], func=ACT.Abs_reciprocal_sqrt,
+            rstds[pair] = stats_pool.tile([P, 2, HEADS], F32, name="rstd", tag="rstd")
+            nc.scalar.activation(out=rstds[pair][:], in_=square_sums[pair][:], func=ACT.Abs_reciprocal_sqrt,
                                  scale=1.0 / (DH * D), bias=EPS / D)
 
-        def vector_multiplies(s):
-            c, b, j = where(s)
-            if c // 2 == 2:
+        def vector_works(s):
+            c, b, j = order[s]
+            if c // 2 == V:
+                if j % 2 == 1:
+                    copy_v(s, "vector")
                 return
+            pair = (c, b, j // 2)
             first_head = (c % 2) * HEADS
-            if s // 2 not in products:
-                products[s // 2] = work.tile([P, 2, HEADS, 2, 2, HALF], F32, name="products", tag="products")
+            if j % 2 == 0:
+                products[pair] = stage.tile([P, 2, HEADS, 2, 2, HALF], F32, name="products", tag="stage")
             for h in range(HEADS):
                 nc.vector.scalar_tensor_tensor(
-                    out=products[s // 2][:, s % 2, h].rearrange("p a s f -> p a (s f)"),
-                    in0=table[:, j, first_head + h], scalar=rstds[s // 2][:, s % 2, h:h + 1],
+                    out=products[pair][:, j % 2, h].rearrange("p o i f -> p o (i f)"),
+                    in0=table[:, j, first_head + h], scalar=rstds[pair][:, j % 2, h:h + 1],
                     in1=sums[s][:, h * DH:(h + 1) * DH].unsqueeze(1).to_broadcast([P, 2, DH]),
                     op0=ALU.mult, op1=ALU.mult)
+            if j == 0:
+                results[(c, b)] = plane_pool.tile([P, HEADS, TILES, DH], F32, name="result", tag="flat", align_bytes=64)
+            result = results[(c, b)]
+            rows = rows_of(c, b)
+            if s >= LAST - 1:
+                one = products[pair][:, j % 2]
+                engine = nc.vector if s == LAST else nc.gpsimd
+                engine.tensor_tensor(out=result[:, :, j, :].rearrange("p h (o f) -> p h o f", f=HALF),
+                                     in0=one[:, :, :, 0, :], in1=one[:, :, :, 1, :], op=ALU.add)
+                nc.sync.dma_start(out=rows[:, :, j, :], in_=result[:, :, j, :])
+            elif j % 2 == 1:
+                nc.gpsimd.tensor_tensor(out=result[:, :, j - 1:j + 1, :].rearrange("p h e (o f) -> p e h o f", f=HALF),
+                                        in0=products[pair][:, :, :, :, 0, :], in1=products[pair][:, :, :, :, 1, :],
+                                        op=ALU.add)
+                nc.sync.dma_start(out=rows[:, :, j - 1:j + 1, :].rearrange("r h j d -> r h (j d)"),
+                                  in_=result[:, :, j - 1:j + 1, :].rearrange("r h j d -> r h (j d)"))
 
-        def vector_sums(s):
-            c, b, j = where(s)
-            if c // 2 == 2:
-                return
-            result = result_tile(s)
-            if s // 2 == LAST_PAIR:
-                one = products[s // 2][:, s % 2]
-                nc.vector.tensor_tensor(out=result[:, :, j, :].rearrange("p h (o f) -> p h o f", f=HALF),
-                                        in0=one[:, :, :, 0, :], in1=one[:, :, :, 1, :], op=ALU.add)
-                store(s)
-                return
-            if s % 2 == 0:
-                return
-            pair = products[s // 2]
-            nc.gpsimd.tensor_tensor(out=result[:, :, j - 1:j + 1, :].rearrange("p h e (o f) -> p e h o f", f=HALF),
-                                    in0=pair[:, :, :, :, 0, :], in1=pair[:, :, :, :, 1, :], op=ALU.add)
-            store(s)
-
-        pieces = []
-        for place in range(HEAD_PLACES, NCHUNK):
-            for g in range(PASSES):
-                for t in range(PACK):
-                    pieces.append(("widen", place, g, t))
-                if place not in ON_VECTOR:
-                    pieces.append(("interleave", place, g, 0))
-            pieces.append(("widened", place, 0, 0))
-        taken = 0
-        vector_later = {}
-        quantized = set(range(HEAD_PLACES))
-
-        for s in range(-AHEAD_TENSOR, NBANK + 1):
-            if 0 <= s + AHEAD_TENSOR < NBANK:
-                assert (s + AHEAD_TENSOR) // BANKS in quantized
+        for s in range(-AHEAD_TENSOR, len(order)):
+            if 0 <= s + AHEAD_TENSOR < len(order):
                 multiply(s + AHEAD_TENSOR)
-            if 0 <= s + AHEAD_SCALAR < NBANK:
+            if 0 <= s + AHEAD_SCALAR < len(order):
                 scalar_reads(s + AHEAD_SCALAR)
-            if 0 <= s < NBANK:
-                planes = 1
-                while taken < len(pieces) and (planes > 0 or pieces[taken][0] != "widen"):
-                    kind, place, g, t = pieces[taken]
-                    taken += 1
-                    if kind == "widen":
-                        widen(place, g, t, "scalar")
-                        planes -= 1
-                    elif kind == "interleave":
-                        interleave_on_scalar(place, g)
-                    elif place in ON_VECTOR:
-                        vector_later[s + 1] = ("interleave", place)
-                        vector_later[s + 3] = ("quantize", place)
-                    else:
-                        vector_later[s + 2] = ("quantize", place)
-                vector_multiplies(s)
-                if s in vector_later:
-                    kind, place = vector_later[s]
-                    if kind == "interleave":
-                        interleave_on_vector(place)
-                    else:
-                        quantize_w(place)
-                        quantized.add(place)
-            if 0 <= s - 1:
-                vector_sums(s - 1)
+            if s >= 0:
+                vector_works(s)

@@ -30,6 +30,7 @@ TILES = N // P
 UNITS = 3
 Q, K, V = 0, 1, 2
 RUN = 4
+FIRST = 8
 AHEAD_TENSOR = 7
 AHEAD_SCALAR = 5
 
@@ -128,8 +129,9 @@ def tile_attn_pa_kernel(tc, x, w_qkv_bytes, w_qkv_scale, scale_param, out_0, out
                                   scales=x_scales[:, b].rearrange("p g c -> p (g c)"),
                                   in_=x_grouped[:, b].rearrange("p g c t -> p (g c t)"))
 
-        position_i = keep.tile([P, TILES], I32, name="position_i")
-        nc.gpsimd.iota(position_i[:], pattern=[[1, TILES]], base=0, channel_multiplier=TILES)
+        position = keep.tile([P, TILES], F32, name="position")
+        nc.gpsimd.iota(position[:], pattern=[[1, TILES]], base=0, channel_multiplier=TILES,
+                       allow_small_or_imprecise_dtypes=True)
         zero = keep.tile([P, 1], F32, name="zero")
         nc.gpsimd.memset(zero[:], 0.0)
         ident = keep.tile([P, P], F32, name="ident")
@@ -137,8 +139,6 @@ def tile_attn_pa_kernel(tc, x, w_qkv_bytes, w_qkv_scale, scale_param, out_0, out
         unused = keep.tile([P, 1], F32, name="unused")
         nc.scalar.activation(out=unused[:], in_=zero[:], func=ACT.Sin)
 
-        position = keep.tile([P, TILES], F32, name="position")
-        nc.vector.tensor_copy(out=position[:], in_=position_i[:])
         freq = keep.tile([P, HALF], F32, name="freq")
         nc.vector.memset(freq[:, 0:1], 1.0)
         width = 1
@@ -146,37 +146,28 @@ def tile_attn_pa_kernel(tc, x, w_qkv_bytes, w_qkv_scale, scale_param, out_0, out
             nc.vector.tensor_scalar(out=freq[:, width:2 * width], in0=freq[:, 0:width],
                                     scalar1=ROPE_BASE ** (-width / HALF), scalar2=None, op0=ALU.mult)
             width *= 2
-        angle = keep.tile([P, TILES, HALF], F32, name="angle")
-        nc.vector.tensor_tensor(out=angle[:], in0=position[:].unsqueeze(2).to_broadcast([P, TILES, HALF]),
-                                in1=freq[:].unsqueeze(1).to_broadcast([P, TILES, HALF]), op=ALU.mult)
         turns = keep.tile([P, 2, TILES, HALF], F32, name="turns")
-        nc.vector.tensor_scalar(out=turns[:, 0], in0=angle[:], scalar1=0.5 / PI, scalar2=0.5,
-                                op0=ALU.mult, op1=ALU.add)
-        nc.vector.tensor_scalar(out=turns[:, 1], in0=angle[:], scalar1=0.5 / PI, scalar2=0.75,
-                                op0=ALU.mult, op1=ALU.add)
-        whole_i = keep.tile([P, 2, TILES, HALF], I32, name="whole_i")
-        nc.vector.tensor_copy(out=whole_i[:], in_=turns[:])
-        whole = keep.tile([P, 2, TILES, HALF], F32, name="whole")
-        nc.vector.tensor_copy(out=whole[:], in_=whole_i[:])
+        nc.vector.scalar_tensor_tensor(out=turns[:, 0], in0=position[:].unsqueeze(2).to_broadcast([P, TILES, HALF]),
+                                       scalar=0.5 / PI, in1=freq[:].unsqueeze(1).to_broadcast([P, TILES, HALF]),
+                                       op0=ALU.mult, op1=ALU.mult)
+        nc.vector.tensor_scalar(out=turns[:, 1], in0=turns[:, 0], scalar1=0.25, scalar2=None, op0=ALU.add)
+        whole = keep.tile([P, 2, TILES, HALF], I32, name="whole")
+        nc.vector.tensor_copy(out=whole[:], in_=turns[:])
         part = keep.tile([P, 2, TILES, HALF], F32, name="part")
         nc.vector.tensor_tensor(out=part[:], in0=turns[:], in1=whole[:], op=ALU.subtract)
-        flat = "p a j f -> p (a j f)"
-        part01 = keep.tile([P, 2, TILES, HALF], F32, name="part01")
-        nc.vector.scalar_tensor_tensor(out=part01[:].rearrange(flat), in0=part[:].rearrange(flat), scalar=0.0,
-                                       in1=part[:].rearrange(flat), op0=ALU.is_lt, op1=ALU.add)
-        reduced = keep.tile([P, 2, TILES, HALF], F32, name="reduced")
-        nc.vector.tensor_scalar(out=reduced[:], in0=part01[:], scalar1=2.0 * PI, scalar2=-PI,
-                                op0=ALU.mult, op1=ALU.add)
-
+        merged = "p a j f -> p (a j f)"
+        folded = keep.tile([P, 2, TILES, HALF], F32, name="folded")
+        nc.vector.scalar_tensor_tensor(out=folded[:].rearrange(merged), in0=part[:].rearrange(merged), scalar=0.5,
+                                       in1=part[:].rearrange(merged), op0=ALU.is_gt, op1=ALU.subtract)
 
         for t in range(PACK):
             widen(Q, 0, t, "scalar")
             widen(Q, 1, t, "vector")
         trig = keep.tile([P, TILES, 2, 2, HALF], F32, name="trig")
-        nc.scalar.activation(out=trig[:, :, 0, 0, :], in_=reduced[:, 1], func=ACT.Sin)
-        nc.scalar.activation(out=trig[:, :, 1, 1, :], in_=reduced[:, 1], func=ACT.Sin)
-        nc.scalar.activation(out=trig[:, :, 1, 0, :], in_=reduced[:, 0], func=ACT.Sin)
-        nc.scalar.activation(out=trig[:, :, 0, 1, :], in_=reduced[:, 0], func=ACT.Sin, scale=-1.0)
+        nc.scalar.activation(out=trig[:, :, 0, 0, :], in_=folded[:, 1], func=ACT.Sin, scale=-2.0 * PI)
+        nc.scalar.activation(out=trig[:, :, 1, 1, :], in_=folded[:, 1], func=ACT.Sin, scale=-2.0 * PI)
+        nc.scalar.activation(out=trig[:, :, 1, 0, :], in_=folded[:, 0], func=ACT.Sin, scale=-2.0 * PI)
+        nc.scalar.activation(out=trig[:, :, 0, 1, :], in_=folded[:, 0], func=ACT.Sin, scale=2.0 * PI)
         nc.scalar.activation(out=unused[:], in_=zero[:], func=ACT.Abs_reciprocal_sqrt, bias=1.0)
 
         def build_table(j):
@@ -210,9 +201,13 @@ def tile_attn_pa_kernel(tc, x, w_qkv_bytes, w_qkv_scale, scale_param, out_0, out
 
         rotated = [(c, b, j) for c in range(4) for b in range(B) for j in range(TILES)]
         plain = [(c, b, j) for c in (4, 5) for b in range(B) for j in range(TILES)]
-        order = []
-        for i in range(len(plain)):
-            order.extend([plain[i], rotated[2 * i], rotated[2 * i + 1]])
+        order = rotated[:FIRST]
+        taken = 0
+        for i in range(FIRST, len(rotated), 2):
+            share = (len(plain) - taken) * 2 // (len(rotated) - i)
+            order.extend(plain[taken:taken + share])
+            taken += share
+            order.extend(rotated[i:i + 2])
         LAST = len(order) - 1
         sums, square_sums, rstds, products, results = {}, {}, {}, {}, {}
 

@@ -31,6 +31,7 @@ UNITS = 3
 Q, K, V = 0, 1, 2
 RUN = 4
 FIRST = 8
+V_ON_VECTOR = ()
 AHEAD_TENSOR = 7
 AHEAD_SCALAR = 5
 
@@ -242,7 +243,7 @@ def tile_attn_pa_kernel(tc, x, w_qkv_bytes, w_qkv_scale, scale_param, out_0, out
         def scalar_reads(s):
             c, b, j = order[s]
             if c // 2 == V:
-                if j % 2 == 0:
+                if j not in V_ON_VECTOR:
                     copy_v(s, "scalar")
                 return
             pair = (c, b, j // 2)
@@ -261,7 +262,7 @@ def tile_attn_pa_kernel(tc, x, w_qkv_bytes, w_qkv_scale, scale_param, out_0, out
         def vector_works(s):
             c, b, j = order[s]
             if c // 2 == V:
-                if j % 2 == 1:
+                if j in V_ON_VECTOR:
                     copy_v(s, "vector")
                 return
             pair = (c, b, j // 2)

@@ -32,6 +32,7 @@ Q, K, V = 0, 1, 2
 RUN = 4
 FIRST = 8
 V_ON_VECTOR = ()
+ALONE = 4
 AHEAD_TENSOR = 7
 AHEAD_SCALAR = 5
 
@@ -51,10 +52,12 @@ def tile_attn_pa_kernel(tc, x, w_qkv_bytes, w_qkv_scale, scale_param, out_0, out
 
         ctx.enter_context(tc.manual_schedule())
 
+        gain_row = keep.tile([P, E], BF16, name="gain_row")
+        nc.vector.memset(gain_row[:].bitcast(I32), 0)
+        ones = keep.tile([P, P], BF16, name="ones")
+        nc.vector.memset(ones[:], 1.0)
         w_scale = keep.tile([P, PASSES, PACK], F32, name="w_scale")
         nc.sync.dma_start(out=w_scale[:], in_=w_qkv_scale.rearrange("(g p t) o -> p g (t o)", p=P, t=PACK))
-        gain = keep.tile([P, E], BF16, name="gain")
-        nc.scalar.dma_start(out=gain[:], in_=scale_param.rearrange("h d -> (h d)").partition_broadcast(P))
         x_raw = [keep.tile([P, TILES, D], BF16, name="x_raw%d" % b) for b in range(B)]
         bytes_view = w_qkv_bytes.rearrange("(g p t) n -> g p t n", p=P, t=PACK)
         w_bytes = {}
@@ -68,6 +71,7 @@ def tile_attn_pa_kernel(tc, x, w_qkv_bytes, w_qkv_scale, scale_param, out_0, out
                 nc.sync.dma_start(out=w_bytes[(u, g)][:], in_=bytes_view[g][:, :, u * E:(u + 1) * E])
 
         load_w(Q)
+        nc.sync.dma_start(out=gain_row[0:1, :], in_=scale_param.rearrange("(o h) d -> o (h d)", o=1))
         load_x(0)
         load_x(1)
         load_w(K)
@@ -97,6 +101,13 @@ def tile_attn_pa_kernel(tc, x, w_qkv_bytes, w_qkv_scale, scale_param, out_0, out
             grouped[(u, g)] = plane_pool.tile([P, E, PACK], BF16, name="grouped", tag="flat", align_bytes=64)
             nc.vector.tensor_copy(out=grouped[(u, g)][:].rearrange("p (c i) t -> p c t i", i=RUN),
                                   in_=wide[(u, g)][:].rearrange("p t (c i) -> p c t i", i=RUN))
+
+        def interleave_on_gpsimd(u, g):
+            grouped[(u, g)] = plane_pool.tile([P, E, PACK], BF16, name="grouped", tag="flat", align_bytes=64)
+            for first in range(0, E, CHUNK):
+                nc.gpsimd.tensor_scalar(out=grouped[(u, g)][:, first:first + CHUNK, :],
+                                        in0=wide[(u, g)][:, :, first:first + CHUNK].rearrange("p t n -> p n t"),
+                                        scalar1=1.0, scalar2=0.0, op0=ALU.mult, op1=ALU.add)
 
         def quantize_w(u, g):
             nc.vector.quantize_mx(out=w_codes[:, u, g, :].bitcast(FP8X4), scales=w_scales[:, u, g, :],
@@ -139,6 +150,11 @@ def tile_attn_pa_kernel(tc, x, w_qkv_bytes, w_qkv_scale, scale_param, out_0, out
         make_identity(nc, ident[:])
         unused = keep.tile([P, 1], F32, name="unused")
         nc.scalar.activation(out=unused[:], in_=zero[:], func=ACT.Sin)
+        gain = []
+        for first in range(0, E, CHUNK):
+            gain.append(psum.tile([P, HEADS, DH], F32, name="gain", tag="bank"))
+            nc.tensor.matmul(out=gain[-1][:].rearrange("p h d -> p (h d)"), lhsT=ones[:],
+                             rhs=gain_row[:, first:first + CHUNK], start=True, stop=True)
 
         freq = keep.tile([P, HALF], F32, name="freq")
         nc.vector.memset(freq[:, 0:1], 1.0)
@@ -161,36 +177,33 @@ def tile_attn_pa_kernel(tc, x, w_qkv_bytes, w_qkv_scale, scale_param, out_0, out
         nc.vector.scalar_tensor_tensor(out=folded[:].rearrange(merged), in0=part[:].rearrange(merged), scalar=0.5,
                                        in1=part[:].rearrange(merged), op0=ALU.is_gt, op1=ALU.subtract)
 
-        for t in range(PACK):
-            widen(Q, 0, t, "scalar")
-            widen(Q, 1, t, "vector")
         trig = keep.tile([P, TILES, 2, 2, HALF], F32, name="trig")
         nc.scalar.activation(out=trig[:, :, 0, 0, :], in_=folded[:, 1], func=ACT.Sin, scale=-2.0 * PI)
         nc.scalar.activation(out=trig[:, :, 1, 1, :], in_=folded[:, 1], func=ACT.Sin, scale=-2.0 * PI)
         nc.scalar.activation(out=trig[:, :, 1, 0, :], in_=folded[:, 0], func=ACT.Sin, scale=-2.0 * PI)
         nc.scalar.activation(out=trig[:, :, 0, 1, :], in_=folded[:, 0], func=ACT.Sin, scale=2.0 * PI)
-        nc.scalar.activation(out=unused[:], in_=zero[:], func=ACT.Abs_reciprocal_sqrt, bias=1.0)
 
         def build_table(j):
             for o in range(2):
-                nc.vector.tensor_tensor(out=table[:, j, :, o, :], in0=gain[:].rearrange("p (h d) -> p h d", d=DH),
-                                        in1=trig[:, j, o].rearrange("p i f -> p (i f)").unsqueeze(1).to_broadcast([P, H, DH]),
-                                        op=ALU.mult)
+                for half in range(H // HEADS):
+                    nc.vector.tensor_tensor(
+                        out=table[:, j, half * HEADS:(half + 1) * HEADS, o, :], in0=gain[half][:],
+                        in1=trig[:, j, o].rearrange("p i f -> p (i f)").unsqueeze(1).to_broadcast([P, HEADS, DH]),
+                        op=ALU.mult)
 
+        for t in range(PACK):
+            widen(Q, 0, t, "scalar")
+            widen(Q, 1, t, "vector")
+        interleave_on_gpsimd(Q, 1)
+        interleave_on_gpsimd(Q, 0)
         transpose_x(0)
         copy_x(0)
+        for j in range(TILES):
+            build_table(j)
         transpose_x(1)
-        copy_x(1)
-        interleave(Q, 1)
-        interleave(Q, 0)
         quantize_w(Q, 1)
         quantize_w(Q, 0)
-        build_table(0)
-        build_table(1)
         quantize_x(0)
-        build_table(2)
-        quantize_x(1)
-        build_table(3)
         for u in (K, V):
             for g in range(PASSES):
                 for t in range(PACK):
@@ -199,6 +212,9 @@ def tile_attn_pa_kernel(tc, x, w_qkv_bytes, w_qkv_scale, scale_param, out_0, out
             interleave(u, 1)
             quantize_w(u, 0)
             quantize_w(u, 1)
+        nc.scalar.activation(out=unused[:], in_=zero[:], func=ACT.Abs_reciprocal_sqrt, bias=1.0)
+        copy_x(1)
+        quantize_x(1)
 
         rotated = [(c, b, j) for c in range(4) for b in range(B) for j in range(TILES)]
         plain = [(c, b, j) for c in (4, 5) for b in range(B) for j in range(TILES)]
@@ -210,6 +226,7 @@ def tile_attn_pa_kernel(tc, x, w_qkv_bytes, w_qkv_scale, scale_param, out_0, out
             taken += share
             order.extend(rotated[i:i + 2])
         LAST = len(order) - 1
+        alone = [s for s in range(len(order)) if order[s] in rotated[-ALONE:]]
         sums, square_sums, rstds, products, results = {}, {}, {}, {}, {}
 
         def multiply(s):
@@ -279,7 +296,7 @@ def tile_attn_pa_kernel(tc, x, w_qkv_bytes, w_qkv_scale, scale_param, out_0, out
                 results[(c, b)] = plane_pool.tile([P, HEADS, TILES, DH], F32, name="result", tag="flat", align_bytes=64)
             result = results[(c, b)]
             rows = rows_of(c, b)
-            if s >= LAST - 1:
+            if s in alone:
                 one = products[pair][:, j % 2]
                 engine = nc.vector if s == LAST else nc.gpsimd
                 engine.tensor_tensor(out=result[:, :, j, :].rearrange("p h (o f) -> p h o f", f=HALF),

@@ -29,10 +29,12 @@ HEADS = CHUNK // DH
 TILES = N // P
 UNITS = 3
 Q, K, V = 0, 1, 2
+SPLIT = 8
 RUN = 4
 FIRST = 8
 V_ON_VECTOR = ()
 ALONE = 4
+ALONE_ON_VECTOR = 2
 AHEAD_TENSOR = 7
 AHEAD_SCALAR = 5
 
@@ -70,7 +72,11 @@ def tile_attn_pa_kernel(tc, x, w_qkv_bytes, w_qkv_scale, scale_param, out_0, out
                 w_bytes[(u, g)] = keep.tile([P, PACK, E], U8, name="w_bytes%d_%d" % (u, g))
                 nc.sync.dma_start(out=w_bytes[(u, g)][:], in_=bytes_view[g][:, :, u * E:(u + 1) * E])
 
-        load_w(Q)
+        for g in range(PASSES):
+            w_bytes[(Q, g)] = keep.tile([P, PACK, E], U8, name="w_bytes%d_%d" % (Q, g))
+        for t in range(0, PACK, 2):
+            for g in range(PASSES):
+                nc.sync.dma_start(out=w_bytes[(Q, g)][:, t:t + 2, :], in_=bytes_view[g][:, t:t + 2, Q * E:(Q + 1) * E])
         nc.sync.dma_start(out=gain_row[0:1, :], in_=scale_param.rearrange("(o h) d -> o (h d)", o=1))
         load_x(0)
         load_x(1)
@@ -156,43 +162,61 @@ def tile_attn_pa_kernel(tc, x, w_qkv_bytes, w_qkv_scale, scale_param, out_0, out
             nc.tensor.matmul(out=gain[-1][:].rearrange("p h d -> p (h d)"), lhsT=ones[:],
                              rhs=gain_row[:, first:first + CHUNK], start=True, stop=True)
 
-        freq = keep.tile([P, HALF], F32, name="freq")
-        nc.vector.memset(freq[:, 0:1], 1.0)
+        fine = keep.tile([P, SPLIT], F32, name="fine")
+        coarse = keep.tile([P, SPLIT], F32, name="coarse")
+        nc.vector.memset(fine[:, 0:1], 1.0)
+        nc.vector.memset(coarse[:, 0:1], 1.0)
         width = 1
-        while width < HALF:
-            nc.vector.tensor_scalar(out=freq[:, width:2 * width], in0=freq[:, 0:width],
+        while width < SPLIT:
+            nc.vector.tensor_scalar(out=fine[:, width:2 * width], in0=fine[:, 0:width],
                                     scalar1=ROPE_BASE ** (-width / HALF), scalar2=None, op0=ALU.mult)
+            nc.vector.tensor_scalar(out=coarse[:, width:2 * width], in0=coarse[:, 0:width],
+                                    scalar1=ROPE_BASE ** (-SPLIT * width / HALF), scalar2=None, op0=ALU.mult)
             width *= 2
-        turns = keep.tile([P, 2, TILES, HALF], F32, name="turns")
-        nc.vector.scalar_tensor_tensor(out=turns[:, 0], in0=position[:].unsqueeze(2).to_broadcast([P, TILES, HALF]),
-                                       scalar=0.5 / PI, in1=freq[:].unsqueeze(1).to_broadcast([P, TILES, HALF]),
+        freq = keep.tile([P, SPLIT, SPLIT], F32, name="freq")
+        nc.vector.tensor_tensor(out=freq[:], in0=coarse[:].unsqueeze(2).to_broadcast([P, SPLIT, SPLIT]),
+                                in1=fine[:].unsqueeze(1).to_broadcast([P, SPLIT, SPLIT]), op=ALU.mult)
+        turns = [keep.tile([P, TILES, HALF], F32, name="turns%d" % a) for a in range(2)]
+        whole = [keep.tile([P, TILES, HALF], I32, name="whole%d" % a) for a in range(2)]
+        part = [keep.tile([P, TILES, HALF], F32, name="part%d" % a) for a in range(2)]
+        folded = [keep.tile([P, TILES, HALF], F32, name="folded%d" % a) for a in range(2)]
+        nc.vector.scalar_tensor_tensor(out=turns[0][:], in0=position[:].unsqueeze(2).to_broadcast([P, TILES, HALF]),
+                                       scalar=0.5 / PI,
+                                       in1=freq[:].rearrange("p a i -> p (a i)").unsqueeze(1).to_broadcast([P, TILES, HALF]),
                                        op0=ALU.mult, op1=ALU.mult)
-        nc.vector.tensor_scalar(out=turns[:, 1], in0=turns[:, 0], scalar1=0.25, scalar2=None, op0=ALU.add)
-        whole = keep.tile([P, 2, TILES, HALF], I32, name="whole")
-        nc.vector.tensor_copy(out=whole[:], in_=turns[:])
-        part = keep.tile([P, 2, TILES, HALF], F32, name="part")
-        nc.vector.tensor_tensor(out=part[:], in0=turns[:], in1=whole[:], op=ALU.subtract)
-        merged = "p a j f -> p (a j f)"
-        folded = keep.tile([P, 2, TILES, HALF], F32, name="folded")
-        nc.vector.scalar_tensor_tensor(out=folded[:].rearrange(merged), in0=part[:].rearrange(merged), scalar=0.5,
-                                       in1=part[:].rearrange(merged), op0=ALU.is_gt, op1=ALU.subtract)
+        nc.vector.tensor_copy(out=whole[0][:], in_=turns[0][:])
+        nc.vector.tensor_scalar(out=turns[1][:], in0=turns[0][:], scalar1=0.25, scalar2=None, op0=ALU.add)
+        nc.vector.tensor_tensor(out=part[0][:], in0=turns[0][:], in1=whole[0][:], op=ALU.subtract)
+        nc.vector.tensor_copy(out=whole[1][:], in_=turns[1][:])
+        merged = "p j f -> p (j f)"
+        nc.vector.scalar_tensor_tensor(out=folded[0][:].rearrange(merged), in0=part[0][:].rearrange(merged), scalar=0.5,
+                                       in1=part[0][:].rearrange(merged), op0=ALU.is_gt, op1=ALU.subtract)
+        nc.vector.tensor_tensor(out=part[1][:], in0=turns[1][:], in1=whole[1][:], op=ALU.subtract)
+        widen(Q, 1, 0, "vector")
+        nc.vector.scalar_tensor_tensor(out=folded[1][:].rearrange(merged), in0=part[1][:].rearrange(merged), scalar=0.5,
+                                       in1=part[1][:].rearrange(merged), op0=ALU.is_gt, op1=ALU.subtract)
 
-        trig = keep.tile([P, TILES, 2, 2, HALF], F32, name="trig")
-        nc.scalar.activation(out=trig[:, :, 0, 0, :], in_=folded[:, 1], func=ACT.Sin, scale=-2.0 * PI)
-        nc.scalar.activation(out=trig[:, :, 1, 1, :], in_=folded[:, 1], func=ACT.Sin, scale=-2.0 * PI)
-        nc.scalar.activation(out=trig[:, :, 1, 0, :], in_=folded[:, 0], func=ACT.Sin, scale=-2.0 * PI)
-        nc.scalar.activation(out=trig[:, :, 0, 1, :], in_=folded[:, 0], func=ACT.Sin, scale=2.0 * PI)
+        trig = keep.tile([P, TILES, 3, HALF], F32, name="trig")
+
+        def take_sine(row, a, sign):
+            nc.scalar.activation(out=trig[:, :, row, :], in_=folded[a][:], func=ACT.Sin, scale=-2.0 * PI * sign)
 
         def build_table(j):
             for o in range(2):
                 for half in range(H // HEADS):
                     nc.vector.tensor_tensor(
                         out=table[:, j, half * HEADS:(half + 1) * HEADS, o, :], in0=gain[half][:],
-                        in1=trig[:, j, o].rearrange("p i f -> p (i f)").unsqueeze(1).to_broadcast([P, HEADS, DH]),
+                        in1=trig[:, j, 1 - o:3 - o].rearrange("p i f -> p (i f)").unsqueeze(1).to_broadcast([P, HEADS, DH]),
                         op=ALU.mult)
 
-        for t in range(PACK):
+        widen(Q, 0, 0, "scalar")
+        take_sine(0, 0, 1.0)
+        take_sine(2, 0, -1.0)
+        widen(Q, 0, 1, "scalar")
+        take_sine(1, 1, 1.0)
+        for t in range(2, PACK):
             widen(Q, 0, t, "scalar")
+        for t in range(1, PACK):
             widen(Q, 1, t, "vector")
         interleave_on_gpsimd(Q, 1)
         interleave_on_gpsimd(Q, 0)
@@ -202,8 +226,8 @@ def tile_attn_pa_kernel(tc, x, w_qkv_bytes, w_qkv_scale, scale_param, out_0, out
             build_table(j)
         transpose_x(1)
         quantize_w(Q, 1)
-        quantize_w(Q, 0)
         quantize_x(0)
+        quantize_w(Q, 0)
         for u in (K, V):
             for g in range(PASSES):
                 for t in range(PACK):
@@ -254,14 +278,24 @@ def tile_attn_pa_kernel(tc, x, w_qkv_bytes, w_qkv_scale, scale_param, out_0, out
             else:
                 nc.vector.tensor_copy(out=result[:, :, j, :], in_=sums[s][:].rearrange("p (h d) -> p h d", d=DH))
             if j == TILES - 1:
-                nc.sync.dma_start(out=rows_of(c, b).rearrange("r h j d -> r h (j d)"),
+                nc.scalar.dma_start(out=rows_of(c, b).rearrange("r h j d -> r h (j d)"),
                                   in_=result[:].rearrange("r h j d -> r h (j d)"))
+
+        waiting = []
+
+        def take_rstd():
+            for pair in waiting:
+                rstds[pair] = stats_pool.tile([P, 2, HEADS], F32, name="rstd", tag="rstd")
+                nc.scalar.activation(out=rstds[pair][:], in_=square_sums[pair][:], func=ACT.Abs_reciprocal_sqrt,
+                                     scale=1.0 / (DH * D), bias=EPS / D)
+            waiting.clear()
 
         def scalar_reads(s):
             c, b, j = order[s]
             if c // 2 == V:
                 if j not in V_ON_VECTOR:
                     copy_v(s, "scalar")
+                take_rstd()
                 return
             pair = (c, b, j // 2)
             if j % 2 == 0:
@@ -270,11 +304,11 @@ def tile_attn_pa_kernel(tc, x, w_qkv_bytes, w_qkv_scale, scale_param, out_0, out
                 squares = scrap.tile([P, DH], BF16, name="squares", tag="squares")
                 nc.scalar.activation(out=squares[:], in_=sums[s][:, h * DH:(h + 1) * DH], func=ACT.Square,
                                      accum_out=square_sums[pair][:, j % 2, h:h + 1])
-            if j % 2 == 0:
-                return
-            rstds[pair] = stats_pool.tile([P, 2, HEADS], F32, name="rstd", tag="rstd")
-            nc.scalar.activation(out=rstds[pair][:], in_=square_sums[pair][:], func=ACT.Abs_reciprocal_sqrt,
-                                 scale=1.0 / (DH * D), bias=EPS / D)
+                take_rstd()
+            if j % 2 == 1:
+                waiting.append(pair)
+            if s == LAST:
+                take_rstd()
 
         def vector_works(s):
             c, b, j = order[s]
@@ -298,7 +332,7 @@ def tile_attn_pa_kernel(tc, x, w_qkv_bytes, w_qkv_scale, scale_param, out_0, out
             rows = rows_of(c, b)
             if s in alone:
                 one = products[pair][:, j % 2]
-                engine = nc.vector if s == LAST else nc.gpsimd
+                engine = nc.vector if s in alone[-ALONE_ON_VECTOR:] else nc.gpsimd
                 engine.tensor_tensor(out=result[:, :, j, :].rearrange("p h (o f) -> p h o f", f=HALF),
                                      in0=one[:, :, :, 0, :], in1=one[:, :, :, 1, :], op=ALU.add)
                 nc.sync.dma_start(out=rows[:, :, j, :], in_=result[:, :, j, :])

@@ -108,12 +108,20 @@ def tile_attn_pa_kernel(tc, x, w_qkv_bytes, w_qkv_scale, scale_param, out_0, out
             nc.vector.tensor_copy(out=grouped[(u, g)][:].rearrange("p (c i) t -> p c t i", i=RUN),
                                   in_=wide[(u, g)][:].rearrange("p t (c i) -> p c t i", i=RUN))
 
-        def interleave_on_gpsimd(u, g):
+        def interleave_on_gpsimd(u, g, chunks):
             grouped[(u, g)] = plane_pool.tile([P, E, PACK], BF16, name="grouped", tag="flat", align_bytes=64)
-            for first in range(0, E, CHUNK):
+            for first in range(0, chunks * CHUNK, CHUNK):
                 nc.gpsimd.tensor_scalar(out=grouped[(u, g)][:, first:first + CHUNK, :],
                                         in0=wide[(u, g)][:, :, first:first + CHUNK].rearrange("p t n -> p n t"),
                                         scalar1=1.0, scalar2=0.0, op0=ALU.mult, op1=ALU.add)
+
+        def interleave_rest(u, g, chunks, engine):
+            out = grouped[(u, g)][:, chunks * CHUNK:E, :].rearrange("p (c i) t -> p c t i", i=RUN)
+            in_ = wide[(u, g)][:, :, chunks * CHUNK:E].rearrange("p t (c i) -> p c t i", i=RUN)
+            if engine == "scalar":
+                nc.scalar.copy(out=out, in_=in_)
+            else:
+                nc.vector.tensor_copy(out=out, in_=in_)
 
         def quantize_w(u, g):
             nc.vector.quantize_mx(out=w_codes[:, u, g, :].bitcast(FP8X4), scales=w_scales[:, u, g, :],
@@ -218,8 +226,8 @@ def tile_attn_pa_kernel(tc, x, w_qkv_bytes, w_qkv_scale, scale_param, out_0, out
             widen(Q, 0, t, "scalar")
         for t in range(1, PACK):
             widen(Q, 1, t, "vector")
-        interleave_on_gpsimd(Q, 1)
-        interleave_on_gpsimd(Q, 0)
+        interleave_on_gpsimd(Q, 1, 2)
+        interleave_on_gpsimd(Q, 0, 1)
         transpose_x(0)
         copy_x(0)
         for j in range(TILES):
@@ -227,6 +235,7 @@ def tile_attn_pa_kernel(tc, x, w_qkv_bytes, w_qkv_scale, scale_param, out_0, out
         transpose_x(1)
         quantize_w(Q, 1)
         quantize_x(0)
+        interleave_rest(Q, 0, 1, "vector")
         quantize_w(Q, 0)
         for u in (K, V):
             for g in range(PASSES):

@@ -34,7 +34,7 @@ RUN = 4
 FIRST = 8
 V_ON_VECTOR = ()
 ALONE = 4
-ALONE_ON_VECTOR = 2
+ALONE_ON_VECTOR = 4
 AHEAD_TENSOR = 7
 AHEAD_SCALAR = 5
 
@@ -319,6 +319,8 @@ def tile_attn_pa_kernel(tc, x, w_qkv_bytes, w_qkv_scale, scale_param, out_0, out
             if s == LAST:
                 take_rstd()
 
+        late = []
+
         def vector_works(s):
             c, b, j = order[s]
             if c // 2 == V:
@@ -340,11 +342,15 @@ def tile_attn_pa_kernel(tc, x, w_qkv_bytes, w_qkv_scale, scale_param, out_0, out
             result = results[(c, b)]
             rows = rows_of(c, b)
             if s in alone:
-                one = products[pair][:, j % 2]
-                engine = nc.vector if s in alone[-ALONE_ON_VECTOR:] else nc.gpsimd
-                engine.tensor_tensor(out=result[:, :, j, :].rearrange("p h (o f) -> p h o f", f=HALF),
-                                     in0=one[:, :, :, 0, :], in1=one[:, :, :, 1, :], op=ALU.add)
-                nc.sync.dma_start(out=rows[:, :, j, :], in_=result[:, :, j, :])
+                late.append((j, products[pair][:, j % 2]))
+                if s in alone[-ALONE_ON_VECTOR:] and s != LAST:
+                    return
+                engine = nc.vector if s == LAST else nc.gpsimd
+                for tile_j, one in late:
+                    engine.tensor_tensor(out=result[:, :, tile_j, :].rearrange("p h (o f) -> p h o f", f=HALF),
+                                         in0=one[:, :, :, 0, :], in1=one[:, :, :, 1, :], op=ALU.add)
+                    nc.sync.dma_start(out=rows[:, :, tile_j, :], in_=result[:, :, tile_j, :])
+                late.clear()
             elif j % 2 == 1:
                 nc.gpsimd.tensor_tensor(out=result[:, :, j - 1:j + 1, :].rearrange("p h e (o f) -> p e h o f", f=HALF),
                                         in0=products[pair][:, :, :, :, 0, :], in1=products[pair][:, :, :, :, 1, :],

@@ -184,30 +184,29 @@ def tile_attn_pa_kernel(tc, x, w_qkv_bytes, w_qkv_scale, scale_param, out_0, out
         freq = keep.tile([P, SPLIT, SPLIT], F32, name="freq")
         nc.vector.tensor_tensor(out=freq[:], in0=coarse[:].unsqueeze(2).to_broadcast([P, SPLIT, SPLIT]),
                                 in1=fine[:].unsqueeze(1).to_broadcast([P, SPLIT, SPLIT]), op=ALU.mult)
-        turns = [keep.tile([P, TILES, HALF], F32, name="turns%d" % a) for a in range(2)]
-        whole = [keep.tile([P, TILES, HALF], I32, name="whole%d" % a) for a in range(2)]
-        part = [keep.tile([P, TILES, HALF], F32, name="part%d" % a) for a in range(2)]
-        folded = [keep.tile([P, TILES, HALF], F32, name="folded%d" % a) for a in range(2)]
-        nc.vector.scalar_tensor_tensor(out=turns[0][:], in0=position[:].unsqueeze(2).to_broadcast([P, TILES, HALF]),
+        turns = keep.tile([P, TILES, HALF], F32, name="turns")
+        whole = keep.tile([P, TILES, HALF], I32, name="whole")
+        part = keep.tile([P, TILES, HALF], F32, name="part")
+        folded = keep.tile([P, TILES, HALF], F32, name="folded")
+        nc.vector.scalar_tensor_tensor(out=turns[:], in0=position[:].unsqueeze(2).to_broadcast([P, TILES, HALF]),
                                        scalar=0.5 / PI,
                                        in1=freq[:].rearrange("p a i -> p (a i)").unsqueeze(1).to_broadcast([P, TILES, HALF]),
                                        op0=ALU.mult, op1=ALU.mult)
-        nc.vector.tensor_copy(out=whole[0][:], in_=turns[0][:])
-        nc.vector.tensor_scalar(out=turns[1][:], in0=turns[0][:], scalar1=0.25, scalar2=None, op0=ALU.add)
-        nc.vector.tensor_tensor(out=part[0][:], in0=turns[0][:], in1=whole[0][:], op=ALU.subtract)
-        nc.vector.tensor_copy(out=whole[1][:], in_=turns[1][:])
+        nc.vector.tensor_copy(out=whole[:], in_=turns[:])
+        nc.vector.tensor_tensor(out=part[:], in0=turns[:], in1=whole[:], op=ALU.subtract)
         merged = "p j f -> p (j f)"
-        nc.vector.scalar_tensor_tensor(out=folded[0][:].rearrange(merged), in0=part[0][:].rearrange(merged), scalar=0.5,
-                                       in1=part[0][:].rearrange(merged), op0=ALU.is_gt, op1=ALU.subtract)
-        nc.vector.tensor_tensor(out=part[1][:], in0=turns[1][:], in1=whole[1][:], op=ALU.subtract)
-        widen(Q, 1, 0, "vector")
-        nc.vector.scalar_tensor_tensor(out=folded[1][:].rearrange(merged), in0=part[1][:].rearrange(merged), scalar=0.5,
-                                       in1=part[1][:].rearrange(merged), op0=ALU.is_gt, op1=ALU.subtract)
+        nc.vector.scalar_tensor_tensor(out=folded[:].rearrange(merged), in0=part[:].rearrange(merged), scalar=0.5,
+                                       in1=part[:].rearrange(merged), op0=ALU.is_gt, op1=ALU.subtract)
 
         trig = keep.tile([P, TILES, 3, HALF], F32, name="trig")
+        distance = keep.tile([P, TILES, HALF], F32, name="distance")
 
-        def take_sine(row, a, sign):
-            nc.scalar.activation(out=trig[:, :, row, :], in_=folded[a][:], func=ACT.Sin, scale=-2.0 * PI * sign)
+        def take_sine(row, sign):
+            nc.scalar.activation(out=trig[:, :, row, :], in_=folded[:], func=ACT.Sin, scale=-2.0 * PI * sign)
+
+        def take_cosine(row):
+            nc.scalar.activation(out=distance[:], in_=folded[:], func=ACT.Abs)
+            nc.scalar.activation(out=trig[:, :, row, :], in_=distance[:], func=ACT.Sin, scale=-2.0 * PI, bias=0.5 * PI)
 
         def build_table(j):
             for o in range(2):
@@ -218,13 +217,12 @@ def tile_attn_pa_kernel(tc, x, w_qkv_bytes, w_qkv_scale, scale_param, out_0, out
                         op=ALU.mult)
 
         widen(Q, 0, 0, "scalar")
-        take_sine(0, 0, 1.0)
-        take_sine(2, 0, -1.0)
-        widen(Q, 0, 1, "scalar")
-        take_sine(1, 1, 1.0)
-        for t in range(2, PACK):
-            widen(Q, 0, t, "scalar")
+        take_sine(0, 1.0)
+        take_sine(2, -1.0)
+        take_cosine(1)
         for t in range(1, PACK):
+            widen(Q, 0, t, "scalar")
+        for t in range(PACK):
             widen(Q, 1, t, "vector")
         interleave_on_gpsimd(Q, 1, 2)
         interleave_on_gpsimd(Q, 0, 1)

@@ -79,8 +79,8 @@ def tile_attn_pa_kernel(tc, x, w_qkv_bytes, w_qkv_scale, scale_param, out_0, out
                 nc.sync.dma_start(out=w_bytes[(Q, g)][:, t:t + 2, :], in_=bytes_view[g][:, t:t + 2, Q * E:(Q + 1) * E])
         nc.sync.dma_start(out=gain_row[0:1, :], in_=scale_param.rearrange("(o h) d -> o (h d)", o=1))
         load_x(0)
-        load_x(1)
         load_w(K)
+        load_x(1)
         load_w(V)
 
         x_grouped = keep.tile([P, B, PASSES, N, PACK], BF16, name="x_grouped", align_bytes=64)
@@ -232,8 +232,8 @@ def tile_attn_pa_kernel(tc, x, w_qkv_bytes, w_qkv_scale, scale_param, out_0, out
             build_table(j)
         transpose_x(1)
         quantize_w(Q, 1)
-        quantize_x(0)
         interleave_rest(Q, 0, 1, "vector")
+        quantize_x(0)
         quantize_w(Q, 0)
         for u in (K, V):
             for g in range(PASSES):
@@ -252,7 +252,8 @@ def tile_attn_pa_kernel(tc, x, w_qkv_bytes, w_qkv_scale, scale_param, out_0, out
         order = rotated[:FIRST]
         taken = 0
         for i in range(FIRST, len(rotated), 2):
-            share = (len(plain) - taken) * 2 // (len(rotated) - i)
+            pairs_so_far = (i - FIRST) // 2 + 1
+            share = len(plain) * pairs_so_far // ((len(rotated) - FIRST) // 2) - taken
             order.extend(plain[taken:taken + share])
             taken += share
             order.extend(rotated[i:i + 2])

@@ -33,7 +33,7 @@ SPLIT = 8
 RUN = 4
 FIRST = 8
 V_ON_VECTOR = ()
-ALONE = 4
+ALONE = 6
 ALONE_ON_VECTOR = 4
 AHEAD_TENSOR = 7
 AHEAD_SCALAR = 5

from contextlib import ExitStack

import concourse.mybir as mybir
from concourse.masks import make_identity

F32 = mybir.dt.float32
BF16 = mybir.dt.bfloat16
U8 = mybir.dt.uint8
U32 = mybir.dt.uint32
I32 = mybir.dt.int32
FP8 = mybir.dt.float8_e4m3fn
FP8X4 = mybir.dt.float8_e4m3fn_x4
ACT = mybir.ActivationFunctionType
ALU = mybir.AluOpType

B, N, D, H, DH = 2, 512, 1024, 8, 128
E = H * DH
HALF = DH // 2
EPS = 1e-6
ROPE_BASE = 10000.0
PI = 3.141592653589793
FLOPS = 2 * B * N * D * 3 * E

P = 128
PACK = 4
PASSES = D // (P * PACK)
CHUNK = 512
HEADS = CHUNK // DH
TILES = N // P
UNITS = 3
Q, K, V = 0, 1, 2
SPLIT = 8
RUN = 4
FIRST = 8
V_ON_VECTOR = ()
ALONE = 6
ALONE_ON_VECTOR = 4
AHEAD_TENSOR = 7
AHEAD_SCALAR = 5


def tile_attn_pa_kernel(tc, x, w_qkv_bytes, w_qkv_scale, scale_param, out_0, out_1, out_2):
    nc = tc.nc
    outs = (out_0, out_1, out_2)

    with ExitStack() as ctx:
        keep = ctx.enter_context(tc.tile_pool(name="keep", bufs=1))
        stage = ctx.enter_context(tc.tile_pool(name="stage", bufs=4))
        plane_pool = ctx.enter_context(tc.tile_pool(name="flat", bufs=3))
        v_pool = ctx.enter_context(tc.tile_pool(name="v_out", bufs=2))
        stats_pool = ctx.enter_context(tc.tile_pool(name="stats", bufs=6))
        scrap = ctx.enter_context(tc.tile_pool(name="scrap", bufs=3))
        psum = ctx.enter_context(tc.psum_pool(name="psum", bufs=8))

        ctx.enter_context(tc.manual_schedule())

        gain_row = keep.tile([P, E], BF16, name="gain_row")
        nc.vector.memset(gain_row[:].bitcast(I32), 0)
        ones = keep.tile([P, P], BF16, name="ones")
        nc.vector.memset(ones[:], 1.0)
        w_scale = keep.tile([P, PASSES, PACK], F32, name="w_scale")
        nc.sync.dma_start(out=w_scale[:], in_=w_qkv_scale.rearrange("(g p t) o -> p g (t o)", p=P, t=PACK))
        x_raw = [keep.tile([P, TILES, D], BF16, name="x_raw%d" % b) for b in range(B)]
        bytes_view = w_qkv_bytes.rearrange("(g p t) n -> g p t n", p=P, t=PACK)
        w_bytes = {}

        def load_x(b):
            nc.sync.dma_start(out=x_raw[b][:], in_=x[b].rearrange("(r j) k -> r j k", j=TILES))

        def load_w(u):
            for g in range(PASSES):
                w_bytes[(u, g)] = keep.tile([P, PACK, E], U8, name="w_bytes%d_%d" % (u, g))
                nc.sync.dma_start(out=w_bytes[(u, g)][:], in_=bytes_view[g][:, :, u * E:(u + 1) * E])

        for g in range(PASSES):
            w_bytes[(Q, g)] = keep.tile([P, PACK, E], U8, name="w_bytes%d_%d" % (Q, g))
        for t in range(0, PACK, 2):
            for g in range(PASSES):
                nc.sync.dma_start(out=w_bytes[(Q, g)][:, t:t + 2, :], in_=bytes_view[g][:, t:t + 2, Q * E:(Q + 1) * E])
        nc.sync.dma_start(out=gain_row[0:1, :], in_=scale_param.rearrange("(o h) d -> o (h d)", o=1))
        load_x(0)
        load_w(K)
        load_x(1)
        load_w(V)

        x_grouped = keep.tile([P, B, PASSES, N, PACK], BF16, name="x_grouped", align_bytes=64)
        x_codes = keep.tile([P, B, PASSES, N], U32, name="x_codes", align_bytes=64)
        x_scales = keep.tile([P, B, PASSES, N], U8, name="x_scales", align_bytes=64)
        w_codes = keep.tile([P, UNITS, PASSES, E], U32, name="w_codes", align_bytes=64)
        w_scales = keep.tile([P, UNITS, PASSES, E], U8, name="w_scales", align_bytes=64)
        table = keep.tile([P, TILES, H, 2, DH], F32, name="table")

        wide = {}
        grouped = {}

        def widen(u, g, t, engine):
            if (u, g) not in wide:
                wide[(u, g)] = stage.tile([P, PACK, E], BF16, name="wide", tag="stage")
            codes = w_bytes[(u, g)][:, t, :].bitcast(FP8)
            if engine == "scalar":
                nc.scalar.activation(out=wide[(u, g)][:, t, :], in_=codes, func=ACT.Copy, scale=w_scale[:, g, t:t + 1])
            else:
                nc.vector.tensor_scalar(out=wide[(u, g)][:, t, :], in0=codes, scalar1=w_scale[:, g, t:t + 1],
                                        scalar2=None, op0=ALU.mult)

        def interleave(u, g):
            grouped[(u, g)] = plane_pool.tile([P, E, PACK], BF16, name="grouped", tag="flat", align_bytes=64)
            nc.vector.tensor_copy(out=grouped[(u, g)][:].rearrange("p (c i) t -> p c t i", i=RUN),
                                  in_=wide[(u, g)][:].rearrange("p t (c i) -> p c t i", i=RUN))

        def interleave_on_gpsimd(u, g, chunks):
            grouped[(u, g)] = plane_pool.tile([P, E, PACK], BF16, name="grouped", tag="flat", align_bytes=64)
            for first in range(0, chunks * CHUNK, CHUNK):
                nc.gpsimd.tensor_scalar(out=grouped[(u, g)][:, first:first + CHUNK, :],
                                        in0=wide[(u, g)][:, :, first:first + CHUNK].rearrange("p t n -> p n t"),
                                        scalar1=1.0, scalar2=0.0, op0=ALU.mult, op1=ALU.add)

        def interleave_rest(u, g, chunks, engine):
            out = grouped[(u, g)][:, chunks * CHUNK:E, :].rearrange("p (c i) t -> p c t i", i=RUN)
            in_ = wide[(u, g)][:, :, chunks * CHUNK:E].rearrange("p t (c i) -> p c t i", i=RUN)
            if engine == "scalar":
                nc.scalar.copy(out=out, in_=in_)
            else:
                nc.vector.tensor_copy(out=out, in_=in_)

        def quantize_w(u, g):
            nc.vector.quantize_mx(out=w_codes[:, u, g, :].bitcast(FP8X4), scales=w_scales[:, u, g, :],
                                  in_=grouped[(u, g)][:].rearrange("p n t -> p (n t)"))

        turned = {}

        def transpose_x(b):
            words = x_raw[b][:].rearrange("r j k -> r (j k)").bitcast(F32)
            per_token = D // 2
            per_pass = per_token // PASSES
            for g in range(PASSES):
                for pair in range(TILES // 2):
                    bank = psum.tile([P, 2, 2, P], F32, name="turned", tag="bank")
                    turned[(b, g, pair)] = bank
                    for e in range(2):
                        start = (2 * pair + e) * per_token + g * per_pass
                        for u in range(2):
                            nc.tensor.transpose(bank[:, e, u, :], words[:, start + u:start + per_pass:2], ident[:])

        def copy_x(b):
            for g in range(PASSES):
                for pair in range(TILES // 2):
                    cols = x_grouped[:, b, g, 2 * pair * P:2 * (pair + 1) * P, :]
                    cols = cols.rearrange("p c t -> p (c t)").bitcast(F32)
                    nc.scalar.copy(out=cols.rearrange("p (e r u) -> p e r u", e=2, u=2),
                                   in_=turned[(b, g, pair)][:].rearrange("p e u r -> p e r u"))

        def quantize_x(b):
            nc.vector.quantize_mx(out=x_codes[:, b].rearrange("p g c -> p (g c)").bitcast(FP8X4),
                                  scales=x_scales[:, b].rearrange("p g c -> p (g c)"),
                                  in_=x_grouped[:, b].rearrange("p g c t -> p (g c t)"))

        position = keep.tile([P, TILES], F32, name="position")
        nc.gpsimd.iota(position[:], pattern=[[1, TILES]], base=0, channel_multiplier=TILES,
                       allow_small_or_imprecise_dtypes=True)
        zero = keep.tile([P, 1], F32, name="zero")
        nc.gpsimd.memset(zero[:], 0.0)
        ident = keep.tile([P, P], F32, name="ident")
        make_identity(nc, ident[:])
        unused = keep.tile([P, 1], F32, name="unused")
        nc.scalar.activation(out=unused[:], in_=zero[:], func=ACT.Sin)
        gain = []
        for first in range(0, E, CHUNK):
            gain.append(psum.tile([P, HEADS, DH], F32, name="gain", tag="bank"))
            nc.tensor.matmul(out=gain[-1][:].rearrange("p h d -> p (h d)"), lhsT=ones[:],
                             rhs=gain_row[:, first:first + CHUNK], start=True, stop=True)

        fine = keep.tile([P, SPLIT], F32, name="fine")
        coarse = keep.tile([P, SPLIT], F32, name="coarse")
        nc.vector.memset(fine[:, 0:1], 1.0)
        nc.vector.memset(coarse[:, 0:1], 1.0)
        width = 1
        while width < SPLIT:
            nc.vector.tensor_scalar(out=fine[:, width:2 * width], in0=fine[:, 0:width],
                                    scalar1=ROPE_BASE ** (-width / HALF), scalar2=None, op0=ALU.mult)
            nc.vector.tensor_scalar(out=coarse[:, width:2 * width], in0=coarse[:, 0:width],
                                    scalar1=ROPE_BASE ** (-SPLIT * width / HALF), scalar2=None, op0=ALU.mult)
            width *= 2
        freq = keep.tile([P, SPLIT, SPLIT], F32, name="freq")
        nc.vector.tensor_tensor(out=freq[:], in0=coarse[:].unsqueeze(2).to_broadcast([P, SPLIT, SPLIT]),
                                in1=fine[:].unsqueeze(1).to_broadcast([P, SPLIT, SPLIT]), op=ALU.mult)
        turns = keep.tile([P, TILES, HALF], F32, name="turns")
        whole = keep.tile([P, TILES, HALF], I32, name="whole")
        part = keep.tile([P, TILES, HALF], F32, name="part")
        folded = keep.tile([P, TILES, HALF], F32, name="folded")
        nc.vector.scalar_tensor_tensor(out=turns[:], in0=position[:].unsqueeze(2).to_broadcast([P, TILES, HALF]),
                                       scalar=0.5 / PI,
                                       in1=freq[:].rearrange("p a i -> p (a i)").unsqueeze(1).to_broadcast([P, TILES, HALF]),
                                       op0=ALU.mult, op1=ALU.mult)
        nc.vector.tensor_copy(out=whole[:], in_=turns[:])
        nc.vector.tensor_tensor(out=part[:], in0=turns[:], in1=whole[:], op=ALU.subtract)
        merged = "p j f -> p (j f)"
        nc.vector.scalar_tensor_tensor(out=folded[:].rearrange(merged), in0=part[:].rearrange(merged), scalar=0.5,
                                       in1=part[:].rearrange(merged), op0=ALU.is_gt, op1=ALU.subtract)

        trig = keep.tile([P, TILES, 3, HALF], F32, name="trig")
        distance = keep.tile([P, TILES, HALF], F32, name="distance")

        def take_sine(row, sign):
            nc.scalar.activation(out=trig[:, :, row, :], in_=folded[:], func=ACT.Sin, scale=-2.0 * PI * sign)

        def take_cosine(row):
            nc.scalar.activation(out=distance[:], in_=folded[:], func=ACT.Abs)
            nc.scalar.activation(out=trig[:, :, row, :], in_=distance[:], func=ACT.Sin, scale=-2.0 * PI, bias=0.5 * PI)

        def build_table(j):
            for o in range(2):
                for half in range(H // HEADS):
                    nc.vector.tensor_tensor(
                        out=table[:, j, half * HEADS:(half + 1) * HEADS, o, :], in0=gain[half][:],
                        in1=trig[:, j, 1 - o:3 - o].rearrange("p i f -> p (i f)").unsqueeze(1).to_broadcast([P, HEADS, DH]),
                        op=ALU.mult)

        widen(Q, 0, 0, "scalar")
        take_sine(0, 1.0)
        take_sine(2, -1.0)
        take_cosine(1)
        for t in range(1, PACK):
            widen(Q, 0, t, "scalar")
        for t in range(PACK):
            widen(Q, 1, t, "vector")
        interleave_on_gpsimd(Q, 1, 2)
        interleave_on_gpsimd(Q, 0, 1)
        transpose_x(0)
        copy_x(0)
        for j in range(TILES):
            build_table(j)
        transpose_x(1)
        quantize_w(Q, 1)
        interleave_rest(Q, 0, 1, "vector")
        quantize_x(0)
        quantize_w(Q, 0)
        for u in (K, V):
            for g in range(PASSES):
                for t in range(PACK):
                    widen(u, g, t, "scalar")
            interleave(u, 0)
            interleave(u, 1)
            quantize_w(u, 0)
            quantize_w(u, 1)
        nc.scalar.activation(out=unused[:], in_=zero[:], func=ACT.Abs_reciprocal_sqrt, bias=1.0)
        copy_x(1)
        quantize_x(1)

        rotated = [(c, b, j) for c in range(4) for b in range(B) for j in range(TILES)]
        plain = [(c, b, j) for c in (4, 5) for b in range(B) for j in range(TILES)]
        order = rotated[:FIRST]
        taken = 0
        for i in range(FIRST, len(rotated), 2):
            pairs_so_far = (i - FIRST) // 2 + 1
            share = len(plain) * pairs_so_far // ((len(rotated) - FIRST) // 2) - taken
            order.extend(plain[taken:taken + share])
            taken += share
            order.extend(rotated[i:i + 2])
        LAST = len(order) - 1
        alone = [s for s in range(len(order)) if order[s] in rotated[-ALONE:]]
        sums, square_sums, rstds, products, results = {}, {}, {}, {}, {}

        def multiply(s):
            c, b, j = order[s]
            columns = slice((c % 2) * CHUNK, (c % 2 + 1) * CHUNK)
            sums[s] = psum.tile([P, CHUNK], F32, name="sums", tag="bank")
            for g in range(PASSES):
                nc.tensor.matmul_mx(out=sums[s][:], lhsT=x_codes[:, b, g, j * P:(j + 1) * P].bitcast(FP8X4),
                                    lhsT_scale=x_scales[:, b, g, j * P:(j + 1) * P],
                                    rhs=w_codes[:, c // 2, g, columns].bitcast(FP8X4),
                                    rhs_scale=w_scales[:, c // 2, g, columns],
                                    start=(g == 0), stop=(g == PASSES - 1))

        def rows_of(c, b):
            first_head = (c % 2) * HEADS
            return outs[c // 2][b, first_head:first_head + HEADS].rearrange("h (r j) d -> r h j d", j=TILES)

        def copy_v(s, engine):
            c, b, j = order[s]
            if j == 0:
                results[(c, b)] = v_pool.tile([P, HEADS, TILES, DH], F32, name="v_result", tag="v_result")
            result = results[(c, b)]
            if engine == "scalar":
                nc.scalar.copy(out=result[:, :, j, :], in_=sums[s][:].rearrange("p (h d) -> p h d", d=DH))
            else:
                nc.vector.tensor_copy(out=result[:, :, j, :], in_=sums[s][:].rearrange("p (h d) -> p h d", d=DH))
            if j == TILES - 1:
                nc.scalar.dma_start(out=rows_of(c, b).rearrange("r h j d -> r h (j d)"),
                                  in_=result[:].rearrange("r h j d -> r h (j d)"))

        waiting = []

        def take_rstd():
            for pair in waiting:
                rstds[pair] = stats_pool.tile([P, 2, HEADS], F32, name="rstd", tag="rstd")
                nc.scalar.activation(out=rstds[pair][:], in_=square_sums[pair][:], func=ACT.Abs_reciprocal_sqrt,
                                     scale=1.0 / (DH * D), bias=EPS / D)
            waiting.clear()

        def scalar_reads(s):
            c, b, j = order[s]
            if c // 2 == V:
                if j not in V_ON_VECTOR:
                    copy_v(s, "scalar")
                take_rstd()
                return
            pair = (c, b, j // 2)
            if j % 2 == 0:
                square_sums[pair] = stats_pool.tile([P, 2, HEADS], F32, name="square_sum", tag="square_sum")
            for h in range(HEADS):
                squares = scrap.tile([P, DH], BF16, name="squares", tag="squares")
                nc.scalar.activation(out=squares[:], in_=sums[s][:, h * DH:(h + 1) * DH], func=ACT.Square,
                                     accum_out=square_sums[pair][:, j % 2, h:h + 1])
                take_rstd()
            if j % 2 == 1:
                waiting.append(pair)
            if s == LAST:
                take_rstd()

        late = []

        def vector_works(s):
            c, b, j = order[s]
            if c // 2 == V:
                if j in V_ON_VECTOR:
                    copy_v(s, "vector")
                return
            pair = (c, b, j // 2)
            first_head = (c % 2) * HEADS
            if j % 2 == 0:
                products[pair] = stage.tile([P, 2, HEADS, 2, 2, HALF], F32, name="products", tag="stage")
            for h in range(HEADS):
                nc.vector.scalar_tensor_tensor(
                    out=products[pair][:, j % 2, h].rearrange("p o i f -> p o (i f)"),
                    in0=table[:, j, first_head + h], scalar=rstds[pair][:, j % 2, h:h + 1],
                    in1=sums[s][:, h * DH:(h + 1) * DH].unsqueeze(1).to_broadcast([P, 2, DH]),
                    op0=ALU.mult, op1=ALU.mult)
            if j == 0:
                results[(c, b)] = plane_pool.tile([P, HEADS, TILES, DH], F32, name="result", tag="flat", align_bytes=64)
            result = results[(c, b)]
            rows = rows_of(c, b)
            if s in alone:
                late.append((j, products[pair][:, j % 2]))
                if s in alone[-ALONE_ON_VECTOR:] and s != LAST:
                    return
                engine = nc.vector if s == LAST else nc.gpsimd
                for tile_j, one in late:
                    engine.tensor_tensor(out=result[:, :, tile_j, :].rearrange("p h (o f) -> p h o f", f=HALF),
                                         in0=one[:, :, :, 0, :], in1=one[:, :, :, 1, :], op=ALU.add)
                    nc.sync.dma_start(out=rows[:, :, tile_j, :], in_=result[:, :, tile_j, :])
                late.clear()
            elif j % 2 == 1:
                nc.gpsimd.tensor_tensor(out=result[:, :, j - 1:j + 1, :].rearrange("p h e (o f) -> p e h o f", f=HALF),
                                        in0=products[pair][:, :, :, :, 0, :], in1=products[pair][:, :, :, :, 1, :],
                                        op=ALU.add)
                nc.sync.dma_start(out=rows[:, :, j - 1:j + 1, :].rearrange("r h j d -> r h (j d)"),
                                  in_=result[:, :, j - 1:j + 1, :].rearrange("r h j d -> r h (j d)"))

        for s in range(-AHEAD_TENSOR, len(order)):
            if 0 <= s + AHEAD_TENSOR < len(order):
                multiply(s + AHEAD_TENSOR)
            if 0 <= s + AHEAD_SCALAR < len(order):
                scalar_reads(s + AHEAD_SCALAR)
            if s >= 0:
                vector_works(s)
